import numpy as np
import ml_dtypes


def mxq(x, axis, fmt="e4m3"):
    dtype, down = {"e4m3": (ml_dtypes.float8_e4m3fn, 7), "e5m2": (ml_dtypes.float8_e5m2, 14)}[fmt]
    v = np.moveaxis(np.asarray(x, np.float32).astype(ml_dtypes.bfloat16).astype(np.float64), axis, -1)
    blocks = v.reshape(v.shape[:-1] + (-1, 32))
    amax = np.abs(blocks).max(-1, keepdims=True)
    byte = np.maximum(np.where(amax > 0, np.frexp(amax)[1] - 1 + 127, 0) - down, 1)
    scale = np.exp2(byte - 127.0)
    codes = (blocks / scale).astype(np.float32).astype(dtype).astype(np.float64)
    return np.moveaxis((codes * scale).reshape(v.shape), -1, axis)


WIDE = False


def mx_kscale(k):
    if not WIDE:
        return np.ones(k)
    levels = np.array([10, -10, 5, -5, 0])
    if k % 512:
        return np.exp2(np.random.permutation(np.resize(levels, k // 32))).repeat(32)
    a = np.empty((k // 512, 16))
    for p in range(k // 512):
        a[p, :8] = np.random.permutation(np.resize(levels, 8))
        for g in range(8):
            far = levels[np.abs(levels - a[p, g]) >= 10]
            a[p, g + 8] = far[np.random.randint(len(far))]
    return np.exp2(a.ravel()).repeat(32)


BF16 = ml_dtypes.bfloat16


def bf(x):
    return np.asarray(x, np.float32).astype(BF16)


def f64(x):
    return np.asarray(x).astype(np.float64)


B, J, C, K, H = 16, 256, 512, 2, 256
KJ = K * J
EPS = 1e-5


def layernorm(v, g, b):
    m = v.mean(-1, keepdims=True)
    var = v.var(-1, keepdims=True)
    return (v - m) / np.sqrt(var + EPS) * g + b


def gcn(xin, adj, spatial_adj, conv_w, conv_b, s_ctx):
    h = (mxq(xin, 2, "e4m3") @ mxq(conv_w, 1, "e4m3").T) + conv_b
    h = h.reshape(B, J, K, C).transpose(0, 2, 1, 3).reshape(B, KJ, C)
    sadj = np.broadcast_to(spatial_adj[None], (B, K - 1, J, J))
    adj4 = np.concatenate([adj * s_ctx, sadj], axis=1).reshape(B, KJ, J)
    return mxq(adj4, 1, "e4m3").transpose(0, 2, 1) @ mxq(h, 1, "e4m3")


def setup_inputs():
    s = mx_kscale(C)
    t = np.sort(mx_kscale(KJ))[np.arange(K) * (KJ - 1) // (K - 1)]
    tw = np.repeat(t, C)
    a = 2.0 / np.sqrt(KJ)
    return {"g1": bf(np.random.standard_normal((B, J, C)) * 0.9 * s),
            "res1": bf(np.random.standard_normal((B, J, C))),
            "adj": bf(np.random.random((B, 1, J, J)) * a / t[0]),
            "spatial_adj": bf(np.random.random((K - 1, J, J)) * a / t[1:, None, None]),
            "conv2_w": bf(np.random.standard_normal((K * C, C)) / np.sqrt(C) / s[None, :] * tw[:, None]),
            "conv2_b": bf(np.random.standard_normal(K * C) * 0.05 * tw),
            "s2": bf(1.5 + 0.1 * np.random.standard_normal(1)),
            "norm2_g": bf(1.0 + 0.1 * np.random.standard_normal(C)),
            "norm2_b": bf(0.1 * np.random.standard_normal(C))}


def reference(g1, res1, adj, spatial_adj, conv2_w, conv2_b, s2, norm2_g, norm2_b):
    g2 = gcn(f64(g1), f64(adj), f64(spatial_adj), f64(conv2_w), f64(conv2_b), f64(s2))
    x2 = f64(res1) + g2
    xn = layernorm(x2, f64(norm2_g), f64(norm2_b))
    return x2, xn

@@ -1,0 +1,461 @@
+from contextlib import ExitStack
+
+import concourse.mybir as mybir
+from concourse.masks import make_identity
+
+F32 = mybir.dt.float32
+BF16 = mybir.dt.bfloat16
+U32 = mybir.dt.uint32
+U8 = mybir.dt.uint8
+I32 = mybir.dt.int32
+FP8X4 = mybir.dt.float8_e4m3fn_x4
+ALU = mybir.AluOpType
+ACT = mybir.ActivationFunctionType
+
+B = 16
+J = 256
+C = 512
+K = 2
+EPS = 1e-5
+P = 128
+HALF = 64
+PACK = 4
+G1_BUFS = 3
+A_BUFS = 2
+S2_COLS = 64
+VECTOR_EVERY = 2
+
+FLOPS = 2 * B * J * C * (K * C) + 2 * B * (K * J) * J * C
+
+
+def tile_block_attention_guide_pb_t_kernel(
+    tc, g1, res1, adj, spatial_adj, conv2_w, conv2_b, s2, norm2_g, norm2_b, out_0, out_1
+):
+    nc = tc.nc
+    with ExitStack() as ctx:
+        consts = ctx.enter_context(tc.tile_pool(name="consts", bufs=1))
+        inputs = ctx.enter_context(tc.tile_pool(name="inputs", bufs=1))
+        stage = ctx.enter_context(tc.tile_pool(name="stage", bufs=2))
+        packed = ctx.enter_context(tc.tile_pool(name="packed", bufs=3))
+        results = ctx.enter_context(tc.tile_pool(name="results", bufs=5))
+        stats = ctx.enter_context(tc.tile_pool(name="stats", bufs=4))
+        psum_turn = ctx.enter_context(tc.psum_pool(name="psum_turn", bufs=2))
+        psum_h = ctx.enter_context(tc.psum_pool(name="psum_h", bufs=4))
+        psum_g2 = ctx.enter_context(tc.psum_pool(name="psum_g2", bufs=2))
+        ctx.enter_context(tc.manual_schedule())
+
+        identity = consts.tile([P, P], F32)
+        make_identity(nc, identity[:])
+        eps = consts.tile([P, 1], F32)
+        nc.vector.memset(eps[:], EPS)
+
+        vector_rows = consts.tile([P, 4 * C + S2_COLS], BF16)
+        nc.vector.memset(vector_rows[:].bitcast(I32), 0)
+        selector = consts.tile([P, P], BF16)
+        nc.vector.memset(selector[:].bitcast(I32), 0)
+        nc.vector.memset(selector[0:1, 0:HALF], 1.0)
+        nc.vector.memset(selector[32:33, HALF:P], 1.0)
+        nc.vector.memset(selector[64:65, :], 1.0)
+        bias_row = conv2_b.rearrange("(o n) -> o n", o=1)
+        nc.scalar.dma_start(out=vector_rows[0:1, 0 : 2 * C], in_=bias_row)
+        nc.scalar.dma_start(out=vector_rows[32:33, 0:C], in_=bias_row[:, C : 2 * C])
+        nc.scalar.dma_start(out=vector_rows[32:33, C : 2 * C], in_=bias_row[:, 0:C])
+        nc.scalar.dma_start(out=vector_rows[64:65, 4 * C : 4 * C + 1], in_=s2.rearrange("(o n) -> o n", o=1))
+        nc.scalar.dma_start(out=vector_rows[64:65, 2 * C : 3 * C], in_=norm2_g.rearrange("(o n) -> o n", o=1))
+        nc.scalar.dma_start(out=vector_rows[64:65, 3 * C : 4 * C], in_=norm2_b.rearrange("(o n) -> o n", o=1))
+        first_sqrt = consts.tile([P, 1], F32)
+        nc.scalar.activation(out=first_sqrt[:], in_=eps[:], func=ACT.Sqrt)
+
+        bias_by_parity = consts.tile([P, 2, C], BF16)
+        gain = consts.tile([P, C], BF16)
+        shift = consts.tile([P, C], BF16)
+        s2_f32 = consts.tile([P, 1], F32)
+
+        def spread_rows():
+            for parity in range(2):
+                spread = psum_h.tile([P, C], F32, tag="h_acc")
+                nc.tensor.matmul(
+                    out=spread[:],
+                    lhsT=selector[:],
+                    rhs=vector_rows[:, parity * C : (parity + 1) * C],
+                    start=True,
+                    stop=True,
+                )
+                nc.vector.tensor_copy(out=bias_by_parity[:, parity, :], in_=spread[:])
+            spread_s2 = psum_g2.tile([P, S2_COLS], F32, tag="g2_acc")
+            nc.tensor.matmul(
+                out=spread_s2[:], lhsT=selector[:], rhs=vector_rows[:, 4 * C :], start=True, stop=True
+            )
+            nc.scalar.copy(out=s2_f32[:], in_=spread_s2[:, 0:1])
+            for n, spread_to in ((2, gain), (3, shift)):
+                spread = psum_h.tile([P, C], F32, tag="h_acc")
+                nc.tensor.matmul(
+                    out=spread[:],
+                    lhsT=selector[:],
+                    rhs=vector_rows[:, n * C : (n + 1) * C],
+                    start=True,
+                    stop=True,
+                )
+                nc.scalar.copy(out=spread_to[:], in_=spread[:])
+
+        g1_codes = [
+            consts.tile([P, 9 * HALF], U32, name="g1_codes%d" % n, align_bytes=64)
+            for n in range(G1_BUFS)
+        ]
+        g1_scales = [
+            consts.tile([P, 9 * HALF], U8, name="g1_scales%d" % n, align_bytes=64)
+            for n in range(G1_BUFS)
+        ]
+        for n in range(G1_BUFS):
+            nc.vector.memset(g1_codes[n][:].bitcast(I32), 0)
+            nc.vector.memset(g1_scales[n][:].bitcast(I32), 0)
+
+        w_raw = consts.tile([P, PACK, K, C], BF16)
+        w_grouped = consts.tile([P, K * C * PACK], BF16, align_bytes=64)
+        w_codes = consts.tile([P, K * C], U32, align_bytes=64)
+        w_scales = consts.tile([P, K * C], U8, align_bytes=64)
+
+        def load_weights():
+            for cc in range(PACK):
+                nc.sync.dma_start(
+                    out=w_raw[:, cc],
+                    in_=conv2_w.rearrange("(k t p) c -> t p k c", k=K, p=P)[cc],
+                )
+
+        def turn_weights():
+            for cc in range(PACK):
+                turned_w = psum_h.tile([P, K, 2, P], F32, tag="h_acc")
+                for k in range(K):
+                    for u in range(2):
+                        nc.tensor.transpose(
+                            turned_w[:, k, u, :],
+                            w_raw[:, cc, k, :].bitcast(F32)[:, u : 2 * P : 2],
+                            identity[:],
+                        )
+                cols = slice(cc * K * P * PACK, (cc + 1) * K * P * PACK)
+                pairs_out = w_grouped[:, cols].bitcast(F32).rearrange("q (k p u) -> q k p u", k=K, u=2)
+                pairs_in = turned_w[:].rearrange("q k u p -> q k p u")
+                if cc % 2 == 0:
+                    nc.vector.tensor_copy(out=pairs_out, in_=pairs_in)
+                else:
+                    nc.scalar.copy(out=pairs_out, in_=pairs_in)
+
+        def quantise_weights():
+            for cc in range(PACK):
+                cols = slice(cc * K * P * PACK, (cc + 1) * K * P * PACK)
+                nc.vector.quantize_mx(
+                    out=w_codes[:, cc * K * P : (cc + 1) * K * P].bitcast(FP8X4),
+                    scales=w_scales[:, cc * K * P : (cc + 1) * K * P],
+                    in_=w_grouped[:, cols],
+                )
+
+        spatial_raw = consts.tile([P, PACK, J], BF16)
+        a_grouped = [
+            consts.tile([P, 2, J, PACK], BF16, name="a_grouped%d" % n, align_bytes=64)
+            for n in range(A_BUFS)
+        ]
+
+        def load_spatial():
+            for half in range(2):
+                nc.sync.dma_start(
+                    out=spatial_raw[half * HALF : (half + 1) * HALF],
+                    in_=spatial_adj[0].rearrange("(r t) w -> r t w", t=PACK),
+                )
+
+        def place_spatial():
+            for n in range(A_BUFS):
+                for parity in range(2):
+                    rows = slice((1 - parity) * HALF, (2 - parity) * HALF)
+                    nc.gpsimd.tensor_scalar(
+                        out=a_grouped[n][rows, parity],
+                        in0=spatial_raw[rows].rearrange("p t w -> p w t"),
+                        scalar1=1.0,
+                        scalar2=0.0,
+                        op0=ALU.mult,
+                        op1=ALU.add,
+                    )
+
+        g1_raw = {}
+        res_raw = {}
+        adj_raw = {}
+        g1_grouped = {}
+        a_codes = {}
+        a_scales = {}
+        h_acc = {}
+        h_grouped = {}
+        h_codes = {}
+        h_scales = {}
+        g2_acc = {}
+        x2 = {}
+        row_sum = {}
+        neg_mean = {}
+        std = {}
+        rstd = {}
+        neg_mean_rstd = {}
+
+        def load_g1(b):
+            g1_raw[b] = inputs.tile([P, 2, C], BF16, name="g1_raw%d" % b)
+            nc.sync.dma_start(out=g1_raw[b][:], in_=g1[b].rearrange("(t p) c -> p t c", p=P))
+
+        def load_adj(pair):
+            adj_raw[pair] = inputs.tile([P, PACK, J], BF16, name="adj_raw%d" % pair)
+            nc.sync.dma_start(
+                out=adj_raw[pair][:],
+                in_=adj[2 * pair : 2 * pair + 2, 0].rearrange("b (r t) w -> (b r) t w", t=PACK),
+            )
+
+        def load_res(b):
+            res_raw[b] = inputs.tile([P, 2, C], BF16, name="res_raw%d" % b)
+            nc.sync.dma_start(out=res_raw[b][:], in_=res1[b].rearrange("(t p) c -> p t c", p=P))
+
+        def turn_g1(b):
+            turned = psum_turn.tile([P, 2, J], F32, tag="turned")
+            for u in range(2):
+                for jt in range(2):
+                    nc.tensor.transpose(
+                        turned[:, u, jt * P : (jt + 1) * P],
+                        g1_raw[b][:, jt, :].bitcast(F32)[:, u : 2 * P : 2],
+                        identity[:],
+                    )
+            grouped = stage.tile([P, J * PACK], BF16, tag="g1_grouped", align_bytes=64)
+            nc.scalar.copy(
+                out=grouped[:].bitcast(F32).rearrange("q (t r u) -> q t r u", t=PACK, u=2),
+                in_=turned[:].rearrange("q u (r t) -> q t r u", t=PACK),
+            )
+            g1_grouped[b] = grouped
+
+        def quantise_g1(b):
+            for t in range(PACK):
+                cols = slice(HALF + t * P, P + t * P)
+                nc.vector.quantize_mx(
+                    out=g1_codes[b % G1_BUFS][:, cols].bitcast(FP8X4),
+                    scales=g1_scales[b % G1_BUFS][:, cols],
+                    in_=g1_grouped[b][:, t * HALF * PACK : (t + 1) * HALF * PACK],
+                )
+
+        def scale_adj(pair):
+            for parity in range(2):
+                rows = slice(parity * HALF, (parity + 1) * HALF)
+                nc.scalar.activation(
+                    out=a_grouped[pair % A_BUFS][rows, parity],
+                    in_=adj_raw[pair][rows].rearrange("p t w -> p w t"),
+                    func=ACT.Copy,
+                    scale=s2_f32[rows, :],
+                )
+
+        def quantise_adj(pair):
+            codes = packed.tile([P, 2 * J], U32, tag="a_codes", align_bytes=64)
+            scales = packed.tile([P, 2 * J], U8, tag="a_scales", align_bytes=64)
+            nc.vector.quantize_mx(
+                out=codes[:].bitcast(FP8X4),
+                scales=scales[:],
+                in_=a_grouped[pair % A_BUFS][:].rearrange("p s w t -> p (s w t)"),
+            )
+            a_codes[pair] = codes
+            a_scales[pair] = scales
+
+        def conv(b, cc):
+            codes = g1_codes[b % G1_BUFS]
+            scales = g1_scales[b % G1_BUFS]
+            k_low = b % 2
+            k_high = 1 - k_low
+            acc = psum_h.tile([P, PACK, P], F32, tag="h_acc")
+            for t in range(PACK):
+                set_then_zero = slice(HALF + t * P, HALF + (t + 1) * P)
+                zero_then_set = slice(t * P, (t + 1) * P)
+                low_cols = slice((K * cc + k_low) * P, (K * cc + k_low + 1) * P)
+                high_cols = slice((K * cc + k_high) * P, (K * cc + k_high + 1) * P)
+                nc.tensor.matmul_mx(
+                    out=acc[:, t, :],
+                    lhsT=codes[:, set_then_zero].bitcast(FP8X4),
+                    lhsT_scale=scales[:, set_then_zero],
+                    rhs=w_codes[:, low_cols].bitcast(FP8X4),
+                    rhs_scale=w_scales[:, low_cols],
+                    start=True,
+                    stop=False,
+                )
+                nc.tensor.matmul_mx(
+                    out=acc[:, t, :],
+                    lhsT=codes[:, zero_then_set].bitcast(FP8X4),
+                    lhsT_scale=scales[:, zero_then_set],
+                    rhs=w_codes[:, high_cols].bitcast(FP8X4),
+                    rhs_scale=w_scales[:, high_cols],
+                    start=False,
+                    stop=True,
+                )
+            h_acc[(b, cc)] = acc
+
+        def add_bias(b, cc):
+            if cc == 0:
+                grouped = stage.tile([P, C, PACK], BF16, tag="h_grouped", align_bytes=64)
+                h_grouped[b] = grouped
+            cols = slice(cc * P, (cc + 1) * P)
+            nc.vector.tensor_tensor(
+                out=h_grouped[b][:, cols, :],
+                in0=h_acc[(b, cc)][:].rearrange("p t c -> p c t"),
+                in1=bias_by_parity[:, b % 2, cols].unsqueeze(2).to_broadcast([P, P, PACK]),
+                op=ALU.add,
+            )
+
+        def quantise_h(b):
+            codes = packed.tile([P, C], U32, tag="h_codes", align_bytes=64)
+            scales = packed.tile([P, C], U8, tag="h_scales", align_bytes=64)
+            nc.vector.quantize_mx(
+                out=codes[:].bitcast(FP8X4),
+                scales=scales[:],
+                in_=h_grouped[b][:].rearrange("p c t -> p (c t)"),
+            )
+            h_codes[b] = codes
+            h_scales[b] = scales
+
+        def aggregate(b):
+            for wt in range(2):
+                cols = slice((b % 2) * J + wt * P, (b % 2) * J + (wt + 1) * P)
+                acc = psum_g2.tile([P, C], F32, tag="g2_acc")
+                nc.tensor.matmul_mx(
+                    out=acc[:],
+                    lhsT=a_codes[b // 2][:, cols].bitcast(FP8X4),
+                    lhsT_scale=a_scales[b // 2][:, cols],
+                    rhs=h_codes[b][:].bitcast(FP8X4),
+                    rhs_scale=h_scales[b][:],
+                    start=True,
+                    stop=True,
+                )
+                g2_acc[(b, wt)] = acc
+
+        def add_residual(b):
+            x2_tile = results.tile([P, 2, C], F32, tag="x2")
+            sums = stats.tile([P, 2], F32, tag="row_sum")
+            for wt in range(2):
+                nc.vector.scalar_tensor_tensor(
+                    out=x2_tile[:, wt, :],
+                    in0=g2_acc[(b, wt)][:],
+                    scalar=1.0,
+                    in1=res_raw[b][:, wt, :],
+                    op0=ALU.mult,
+                    op1=ALU.add,
+                    accum_out=sums[:, wt : wt + 1],
+                )
+            nc.sync.dma_start(out=out_0[b].rearrange("(t p) c -> p t c", p=P), in_=x2_tile[:])
+            x2[b] = x2_tile
+            row_sum[b] = sums
+
+        def deviation(b):
+            minus_mean = stats.tile([P, 2], F32, tag="neg_mean")
+            nc.scalar.activation(out=minus_mean[:], in_=row_sum[b][:], func=ACT.Copy, scale=-1.0 / C)
+            squares = stats.tile([P, 2], F32, tag="squares")
+            for wt in range(2):
+                unread = stats.tile([P, C], BF16, tag="unread")
+                nc.scalar.activation(
+                    out=unread[:],
+                    in_=x2[b][:, wt, :],
+                    func=ACT.Square,
+                    bias=minus_mean[:, wt : wt + 1],
+                    scale=1.0,
+                    accum_out=squares[:, wt : wt + 1],
+                )
+            deviation_tile = stats.tile([P, 2], F32, tag="std")
+            nc.scalar.activation(
+                out=deviation_tile[:], in_=squares[:], func=ACT.Sqrt, bias=eps[:], scale=1.0 / C
+            )
+            neg_mean[b] = minus_mean
+            std[b] = deviation_tile
+
+        def invert_deviation(b):
+            inverse = stats.tile([P, 2], F32, tag="rstd")
+            nc.vector.reciprocal(out=inverse[:], in_=std[b][:])
+            rstd[b] = inverse
+            if b % VECTOR_EVERY != VECTOR_EVERY - 1:
+                offset = stats.tile([P, 2], F32, tag="neg_mean_rstd")
+                nc.vector.tensor_tensor(
+                    out=offset[:], in0=neg_mean[b][:], in1=inverse[:], op=ALU.mult
+                )
+                neg_mean_rstd[b] = offset
+
+        def normalise(b):
+            xn = results.tile([P, 2, C], F32, tag="xn")
+            if b % VECTOR_EVERY != VECTOR_EVERY - 1:
+                for wt in range(2):
+                    nc.scalar.activation(
+                        out=xn[:, wt, :],
+                        in_=x2[b][:, wt, :],
+                        func=ACT.Identity,
+                        bias=neg_mean_rstd[b][:, wt : wt + 1],
+                        scale=rstd[b][:, wt : wt + 1],
+                    )
+                nc.gpsimd.tensor_tensor(
+                    out=xn[:], in0=xn[:], in1=gain[:].unsqueeze(1).to_broadcast([P, 2, C]), op=ALU.mult
+                )
+                nc.gpsimd.tensor_tensor(
+                    out=xn[:], in0=xn[:], in1=shift[:].unsqueeze(1).to_broadcast([P, 2, C]), op=ALU.add
+                )
+            else:
+                for wt in range(2):
+                    nc.vector.scalar_tensor_tensor(
+                        out=xn[:, wt, :],
+                        in0=x2[b][:, wt, :],
+                        scalar=neg_mean[b][:, wt : wt + 1],
+                        in1=gain[:],
+                        op0=ALU.add,
+                        op1=ALU.mult,
+                    )
+                for wt in range(2):
+                    nc.vector.scalar_tensor_tensor(
+                        out=xn[:, wt, :],
+                        in0=xn[:, wt, :],
+                        scalar=rstd[b][:, wt : wt + 1],
+                        in1=shift[:],
+                        op0=ALU.mult,
+                        op1=ALU.add,
+                    )
+            nc.sync.dma_start(out=out_1[b].rearrange("(t p) c -> p t c", p=P), in_=xn[:])
+
+        def in_range(b):
+            return 0 <= b < B
+
+        def step(i):
+            for cc in range(PACK):
+                if in_range(i):
+                    add_bias(i, cc)
+                if in_range(i + 1):
+                    conv(i + 1, cc)
+            if in_range(i - 1):
+                add_residual(i - 1)
+            if in_range(i - 2):
+                invert_deviation(i - 2)
+            if in_range(i):
+                if i % 2 == 0:
+                    quantise_adj(i // 2)
+                quantise_h(i)
+                aggregate(i)
+            if in_range(i + 2):
+                quantise_g1(i + 2)
+            if in_range(i - 1):
+                deviation(i - 1)
+            if in_range(i - 2):
+                normalise(i - 2)
+            if in_range(i + 3):
+                turn_g1(i + 3)
+            if in_range(i + 2) and i % 2 == 0:
+                scale_adj((i + 2) // 2)
+
+        load_g1(0)
+        load_weights()
+        load_adj(0)
+        load_spatial()
+        for b in range(1, B + 4):
+            if in_range(b):
+                load_g1(b)
+                if b % 2 == 0:
+                    load_adj(b // 2)
+            if in_range(b - 4):
+                load_res(b - 4)
+
+        spread_rows()
+        step(-3)
+        turn_weights()
+        step(-2)
+        quantise_weights()
+        place_spatial()
+        for i in range(-1, B + 2):
+            step(i)

@@ -18,12 +18,11 @@ C = 512
 K = 2
 EPS = 1e-5
 P = 128
-HALF = 64
+PAIRS = B // 2
+HALF = P // 2
 PACK = 4
-G1_BUFS = 3
-A_BUFS = 2
+CHUNKS = C // P
 S2_COLS = 64
-VECTOR_EVERY = 2
 
 FLOPS = 2 * B * J * C * (K * C) + 2 * B * (K * J) * J * C
 
@@ -37,8 +36,8 @@ def tile_block_attention_guide_pb_t_kernel(
         inputs = ctx.enter_context(tc.tile_pool(name="inputs", bufs=1))
         stage = ctx.enter_context(tc.tile_pool(name="stage", bufs=2))
         packed = ctx.enter_context(tc.tile_pool(name="packed", bufs=3))
-        results = ctx.enter_context(tc.tile_pool(name="results", bufs=5))
-        stats = ctx.enter_context(tc.tile_pool(name="stats", bufs=4))
+        results = ctx.enter_context(tc.tile_pool(name="results", bufs=6))
+        stats = ctx.enter_context(tc.tile_pool(name="stats", bufs=6))
         psum_turn = ctx.enter_context(tc.psum_pool(name="psum_turn", bufs=2))
         psum_h = ctx.enter_context(tc.psum_pool(name="psum_h", bufs=4))
         psum_g2 = ctx.enter_context(tc.psum_pool(name="psum_g2", bufs=2))
@@ -51,134 +50,128 @@ def tile_block_attention_guide_pb_t_kernel(
 
         vector_rows = consts.tile([P, 4 * C + S2_COLS], BF16)
         nc.vector.memset(vector_rows[:].bitcast(I32), 0)
-        selector = consts.tile([P, P], BF16)
-        nc.vector.memset(selector[:].bitcast(I32), 0)
-        nc.vector.memset(selector[0:1, 0:HALF], 1.0)
-        nc.vector.memset(selector[32:33, HALF:P], 1.0)
-        nc.vector.memset(selector[64:65, :], 1.0)
-        bias_row = conv2_b.rearrange("(o n) -> o n", o=1)
-        nc.scalar.dma_start(out=vector_rows[0:1, 0 : 2 * C], in_=bias_row)
-        nc.scalar.dma_start(out=vector_rows[32:33, 0:C], in_=bias_row[:, C : 2 * C])
-        nc.scalar.dma_start(out=vector_rows[32:33, C : 2 * C], in_=bias_row[:, 0:C])
-        nc.scalar.dma_start(out=vector_rows[64:65, 4 * C : 4 * C + 1], in_=s2.rearrange("(o n) -> o n", o=1))
-        nc.scalar.dma_start(out=vector_rows[64:65, 2 * C : 3 * C], in_=norm2_g.rearrange("(o n) -> o n", o=1))
-        nc.scalar.dma_start(out=vector_rows[64:65, 3 * C : 4 * C], in_=norm2_b.rearrange("(o n) -> o n", o=1))
+        ones = consts.tile([P, P], BF16)
+        nc.vector.memset(ones[:], 1.0)
+        nc.scalar.dma_start(out=vector_rows[0:1, 0 : 2 * C], in_=conv2_b.rearrange("(o n) -> o n", o=1))
+        nc.scalar.dma_start(out=vector_rows[0:1, 4 * C : 4 * C + 1], in_=s2.rearrange("(o n) -> o n", o=1))
+        nc.scalar.dma_start(out=vector_rows[0:1, 2 * C : 3 * C], in_=norm2_g.rearrange("(o n) -> o n", o=1))
+        nc.scalar.dma_start(out=vector_rows[0:1, 3 * C : 4 * C], in_=norm2_b.rearrange("(o n) -> o n", o=1))
         first_sqrt = consts.tile([P, 1], F32)
         nc.scalar.activation(out=first_sqrt[:], in_=eps[:], func=ACT.Sqrt)
 
-        bias_by_parity = consts.tile([P, 2, C], BF16)
+        bias = consts.tile([P, K * C], BF16)
         gain = consts.tile([P, C], BF16)
         shift = consts.tile([P, C], BF16)
         s2_f32 = consts.tile([P, 1], F32)
 
         def spread_rows():
-            for parity in range(2):
+            for k in range(K):
                 spread = psum_h.tile([P, C], F32, tag="h_acc")
                 nc.tensor.matmul(
-                    out=spread[:],
-                    lhsT=selector[:],
-                    rhs=vector_rows[:, parity * C : (parity + 1) * C],
-                    start=True,
-                    stop=True,
+                    out=spread[:], lhsT=ones[:], rhs=vector_rows[:, k * C : (k + 1) * C], start=True, stop=True
                 )
-                nc.vector.tensor_copy(out=bias_by_parity[:, parity, :], in_=spread[:])
+                nc.vector.tensor_copy(out=bias[:, k * C : (k + 1) * C], in_=spread[:])
             spread_s2 = psum_g2.tile([P, S2_COLS], F32, tag="g2_acc")
             nc.tensor.matmul(
-                out=spread_s2[:], lhsT=selector[:], rhs=vector_rows[:, 4 * C :], start=True, stop=True
+                out=spread_s2[:], lhsT=ones[:], rhs=vector_rows[:, 4 * C :], start=True, stop=True
             )
             nc.scalar.copy(out=s2_f32[:], in_=spread_s2[:, 0:1])
             for n, spread_to in ((2, gain), (3, shift)):
                 spread = psum_h.tile([P, C], F32, tag="h_acc")
                 nc.tensor.matmul(
-                    out=spread[:],
-                    lhsT=selector[:],
-                    rhs=vector_rows[:, n * C : (n + 1) * C],
-                    start=True,
-                    stop=True,
+                    out=spread[:], lhsT=ones[:], rhs=vector_rows[:, n * C : (n + 1) * C], start=True, stop=True
                 )
                 nc.scalar.copy(out=spread_to[:], in_=spread[:])
 
-        g1_codes = [
-            consts.tile([P, 9 * HALF], U32, name="g1_codes%d" % n, align_bytes=64)
-            for n in range(G1_BUFS)
-        ]
-        g1_scales = [
-            consts.tile([P, 9 * HALF], U8, name="g1_scales%d" % n, align_bytes=64)
-            for n in range(G1_BUFS)
-        ]
-        for n in range(G1_BUFS):
-            nc.vector.memset(g1_codes[n][:].bitcast(I32), 0)
-            nc.vector.memset(g1_scales[n][:].bitcast(I32), 0)
-
-        w_raw = consts.tile([P, PACK, K, C], BF16)
+        W_PARTS = 4
+        W_COLS = K * C // W_PARTS
+        w_raw = consts.tile([P, W_PARTS, 2, C], BF16)
         w_grouped = consts.tile([P, K * C * PACK], BF16, align_bytes=64)
         w_codes = consts.tile([P, K * C], U32, align_bytes=64)
         w_scales = consts.tile([P, K * C], U8, align_bytes=64)
 
         def load_weights():
-            for cc in range(PACK):
+            for n in range(W_PARTS):
                 nc.sync.dma_start(
-                    out=w_raw[:, cc],
-                    in_=conv2_w.rearrange("(k t p) c -> t p k c", k=K, p=P)[cc],
+                    out=w_raw[:, n],
+                    in_=conv2_w.rearrange("(n m p) c -> n p m c", n=W_PARTS, p=P)[n],
                 )
 
         def turn_weights():
-            for cc in range(PACK):
-                turned_w = psum_h.tile([P, K, 2, P], F32, tag="h_acc")
-                for k in range(K):
+            for n in range(W_PARTS):
+                turned_w = psum_h.tile([P, 2, 2, P], F32, tag="h_acc")
+                for m in range(2):
                     for u in range(2):
                         nc.tensor.transpose(
-                            turned_w[:, k, u, :],
-                            w_raw[:, cc, k, :].bitcast(F32)[:, u : 2 * P : 2],
+                            turned_w[:, m, u, :],
+                            w_raw[:, n, m, :].bitcast(F32)[:, u : 2 * P : 2],
                             identity[:],
                         )
-                cols = slice(cc * K * P * PACK, (cc + 1) * K * P * PACK)
-                pairs_out = w_grouped[:, cols].bitcast(F32).rearrange("q (k p u) -> q k p u", k=K, u=2)
-                pairs_in = turned_w[:].rearrange("q k u p -> q k p u")
-                if cc % 2 == 0:
-                    nc.vector.tensor_copy(out=pairs_out, in_=pairs_in)
+                cols = slice(n * W_COLS * PACK, (n + 1) * W_COLS * PACK)
+                words_out = w_grouped[:, cols].bitcast(F32).rearrange("q (m p u) -> q m p u", m=2, u=2)
+                words_in = turned_w[:].rearrange("q m u p -> q m p u")
+                if n % 2 == 0:
+                    nc.vector.tensor_copy(out=words_out, in_=words_in)
                 else:
-                    nc.scalar.copy(out=pairs_out, in_=pairs_in)
+                    nc.scalar.copy(out=words_out, in_=words_in)
 
         def quantise_weights():
-            for cc in range(PACK):
-                cols = slice(cc * K * P * PACK, (cc + 1) * K * P * PACK)
+            for k in range(K):
                 nc.vector.quantize_mx(
-                    out=w_codes[:, cc * K * P : (cc + 1) * K * P].bitcast(FP8X4),
-                    scales=w_scales[:, cc * K * P : (cc + 1) * K * P],
-                    in_=w_grouped[:, cols],
+                    out=w_codes[:, k * C : (k + 1) * C].bitcast(FP8X4),
+                    scales=w_scales[:, k * C : (k + 1) * C],
+                    in_=w_grouped[:, k * C * PACK : (k + 1) * C * PACK],
                 )
 
-        spatial_raw = consts.tile([P, PACK, J], BF16)
         a_grouped = [
-            consts.tile([P, 2, J, PACK], BF16, name="a_grouped%d" % n, align_bytes=64)
-            for n in range(A_BUFS)
+            consts.tile([P, 2, J, PACK], BF16, name="a_grouped%d" % n, align_bytes=64) for n in range(2)
         ]
+        spatial_raw = consts.tile([P, PACK, J], BF16)
+        spatial_grouped = consts.tile([P, 2, J, PACK], BF16, align_bytes=64)
+        spatial_codes = consts.tile([P, 2 * J], U32, align_bytes=64)
+        spatial_scales = consts.tile([P, 2 * J], U8, align_bytes=64)
+
+        def own_rows(s):
+            return slice(s * HALF, (s + 1) * HALF)
+
+        def zero_other_rows():
+            for tile in (spatial_grouped, a_grouped[0], a_grouped[1]):
+                for s in range(2):
+                    nc.gpsimd.memset(tile[own_rows(1 - s), s].rearrange("p w t -> p (w t)").bitcast(I32), 0)
 
         def load_spatial():
-            for half in range(2):
+            for s in range(2):
                 nc.sync.dma_start(
-                    out=spatial_raw[half * HALF : (half + 1) * HALF],
+                    out=spatial_raw[own_rows(s)],
                     in_=spatial_adj[0].rearrange("(r t) w -> r t w", t=PACK),
                 )
 
         def place_spatial():
-            for n in range(A_BUFS):
-                for parity in range(2):
-                    rows = slice((1 - parity) * HALF, (2 - parity) * HALF)
-                    nc.gpsimd.tensor_scalar(
-                        out=a_grouped[n][rows, parity],
-                        in0=spatial_raw[rows].rearrange("p t w -> p w t"),
-                        scalar1=1.0,
-                        scalar2=0.0,
-                        op0=ALU.mult,
-                        op1=ALU.add,
-                    )
+            for s in range(2):
+                rows = own_rows(s)
+                nc.gpsimd.tensor_scalar(
+                    out=spatial_grouped[rows, s].rearrange("p (wt m) t -> p wt m t", wt=2),
+                    in0=spatial_raw[rows].rearrange("p t (m wt) -> p wt m t", wt=2),
+                    scalar1=1.0,
+                    scalar2=0.0,
+                    op0=ALU.mult,
+                    op1=ALU.add,
+                )
+
+        def quantise_spatial():
+            nc.vector.quantize_mx(
+                out=spatial_codes[:].bitcast(FP8X4),
+                scales=spatial_scales[:],
+                in_=spatial_grouped[:].rearrange("p s w t -> p (s w t)"),
+            )
 
         g1_raw = {}
         res_raw = {}
         adj_raw = {}
+        g1_turned = {}
         g1_grouped = {}
+        g1_codes = {}
+        g1_scales = {}
         a_codes = {}
         a_scales = {}
         h_acc = {}
@@ -193,162 +186,161 @@ def tile_block_attention_guide_pb_t_kernel(
         rstd = {}
         neg_mean_rstd = {}
 
-        def load_g1(b):
-            g1_raw[b] = inputs.tile([P, 2, C], BF16, name="g1_raw%d" % b)
-            nc.sync.dma_start(out=g1_raw[b][:], in_=g1[b].rearrange("(t p) c -> p t c", p=P))
-
-        def load_adj(pair):
-            adj_raw[pair] = inputs.tile([P, PACK, J], BF16, name="adj_raw%d" % pair)
+        def load_g1(i):
+            g1_raw[i] = inputs.tile([P, PACK, C], BF16, name="g1_raw%d" % i)
             nc.sync.dma_start(
-                out=adj_raw[pair][:],
-                in_=adj[2 * pair : 2 * pair + 2, 0].rearrange("b (r t) w -> (b r) t w", t=PACK),
+                out=g1_raw[i][:], in_=g1[2 * i : 2 * i + 2].rearrange("b (r t) c -> (b r) t c", t=PACK)
             )
 
-        def load_res(b):
-            res_raw[b] = inputs.tile([P, 2, C], BF16, name="res_raw%d" % b)
-            nc.sync.dma_start(out=res_raw[b][:], in_=res1[b].rearrange("(t p) c -> p t c", p=P))
-
-        def turn_g1(b):
-            turned = psum_turn.tile([P, 2, J], F32, tag="turned")
-            for u in range(2):
-                for jt in range(2):
-                    nc.tensor.transpose(
-                        turned[:, u, jt * P : (jt + 1) * P],
-                        g1_raw[b][:, jt, :].bitcast(F32)[:, u : 2 * P : 2],
-                        identity[:],
-                    )
-            grouped = stage.tile([P, J * PACK], BF16, tag="g1_grouped", align_bytes=64)
-            nc.scalar.copy(
-                out=grouped[:].bitcast(F32).rearrange("q (t r u) -> q t r u", t=PACK, u=2),
-                in_=turned[:].rearrange("q u (r t) -> q t r u", t=PACK),
+        def load_adj(i):
+            adj_raw[i] = inputs.tile([P, PACK, J], BF16, name="adj_raw%d" % i)
+            nc.sync.dma_start(
+                out=adj_raw[i][:], in_=adj[2 * i : 2 * i + 2, 0].rearrange("b (r t) w -> (b r) t w", t=PACK)
             )
-            g1_grouped[b] = grouped
 
-        def quantise_g1(b):
-            for t in range(PACK):
-                cols = slice(HALF + t * P, P + t * P)
-                nc.vector.quantize_mx(
-                    out=g1_codes[b % G1_BUFS][:, cols].bitcast(FP8X4),
-                    scales=g1_scales[b % G1_BUFS][:, cols],
-                    in_=g1_grouped[b][:, t * HALF * PACK : (t + 1) * HALF * PACK],
+        def load_res(i):
+            res_raw[i] = inputs.tile([P, 2, 2, C], BF16, name="res_raw%d" % i)
+            for s in range(2):
+                nc.sync.dma_start(
+                    out=res_raw[i][:, s], in_=res1[2 * i + s].rearrange("(m wt) c -> m wt c", wt=2)
                 )
 
-        def scale_adj(pair):
-            for parity in range(2):
-                rows = slice(parity * HALF, (parity + 1) * HALF)
+        def turn_g1(i):
+            g1_turned[i] = []
+            for half in range(2):
+                turned = psum_turn.tile([P, 2, 2, P], F32, tag="turned")
+                for t in range(2):
+                    for u in range(2):
+                        nc.tensor.transpose(
+                            turned[:, t, u, :],
+                            g1_raw[i][:, 2 * half + t, :].bitcast(F32)[:, u : 2 * P : 2],
+                            identity[:],
+                        )
+                g1_turned[i].append(turned)
+
+        def group_g1(i):
+            grouped = stage.tile([P, PACK * P * PACK], BF16, tag="g1_grouped", align_bytes=64)
+            for half in range(2):
+                cols = slice(half * 2 * P * PACK, (half + 1) * 2 * P * PACK)
+                nc.scalar.copy(
+                    out=grouped[:, cols].bitcast(F32).rearrange("q (t n u) -> q t n u", t=2, u=2),
+                    in_=g1_turned[i][half][:].rearrange("q t u n -> q t n u"),
+                )
+            g1_grouped[i] = grouped
+
+        def quantise_g1(i):
+            codes = packed.tile([P, PACK * P], U32, tag="g1_codes", align_bytes=64)
+            scales = packed.tile([P, PACK * P], U8, tag="g1_scales", align_bytes=64)
+            nc.vector.quantize_mx(out=codes[:].bitcast(FP8X4), scales=scales[:], in_=g1_grouped[i][:])
+            g1_codes[i] = codes
+            g1_scales[i] = scales
+
+        def scale_adj(i):
+            for s in range(2):
+                rows = own_rows(s)
                 nc.scalar.activation(
-                    out=a_grouped[pair % A_BUFS][rows, parity],
-                    in_=adj_raw[pair][rows].rearrange("p t w -> p w t"),
+                    out=a_grouped[i % 2][rows, s].rearrange("p (wt m) t -> p wt m t", wt=2),
+                    in_=adj_raw[i][rows].rearrange("p t (m wt) -> p wt m t", wt=2),
                     func=ACT.Copy,
                     scale=s2_f32[rows, :],
                 )
 
-        def quantise_adj(pair):
+        def quantise_adj(i):
             codes = packed.tile([P, 2 * J], U32, tag="a_codes", align_bytes=64)
             scales = packed.tile([P, 2 * J], U8, tag="a_scales", align_bytes=64)
             nc.vector.quantize_mx(
                 out=codes[:].bitcast(FP8X4),
                 scales=scales[:],
-                in_=a_grouped[pair % A_BUFS][:].rearrange("p s w t -> p (s w t)"),
+                in_=a_grouped[i % 2][:].rearrange("p s w t -> p (s w t)"),
             )
-            a_codes[pair] = codes
-            a_scales[pair] = scales
+            a_codes[i] = codes
+            a_scales[i] = scales
 
-        def conv(b, cc):
-            codes = g1_codes[b % G1_BUFS]
-            scales = g1_scales[b % G1_BUFS]
-            k_low = b % 2
-            k_high = 1 - k_low
+        def conv(i, k, cc):
             acc = psum_h.tile([P, PACK, P], F32, tag="h_acc")
+            w_cols = slice(k * C + cc * P, k * C + (cc + 1) * P)
             for t in range(PACK):
-                set_then_zero = slice(HALF + t * P, HALF + (t + 1) * P)
-                zero_then_set = slice(t * P, (t + 1) * P)
-                low_cols = slice((K * cc + k_low) * P, (K * cc + k_low + 1) * P)
-                high_cols = slice((K * cc + k_high) * P, (K * cc + k_high + 1) * P)
+                cols = slice(t * P, (t + 1) * P)
                 nc.tensor.matmul_mx(
                     out=acc[:, t, :],
-                    lhsT=codes[:, set_then_zero].bitcast(FP8X4),
-                    lhsT_scale=scales[:, set_then_zero],
-                    rhs=w_codes[:, low_cols].bitcast(FP8X4),
-                    rhs_scale=w_scales[:, low_cols],
+                    lhsT=g1_codes[i][:, cols].bitcast(FP8X4),
+                    lhsT_scale=g1_scales[i][:, cols],
+                    rhs=w_codes[:, w_cols].bitcast(FP8X4),
+                    rhs_scale=w_scales[:, w_cols],
                     start=True,
-                    stop=False,
-                )
-                nc.tensor.matmul_mx(
-                    out=acc[:, t, :],
-                    lhsT=codes[:, zero_then_set].bitcast(FP8X4),
-                    lhsT_scale=scales[:, zero_then_set],
-                    rhs=w_codes[:, high_cols].bitcast(FP8X4),
-                    rhs_scale=w_scales[:, high_cols],
-                    start=False,
                     stop=True,
                 )
-            h_acc[(b, cc)] = acc
+            h_acc[(i, k, cc)] = acc
 
-        def add_bias(b, cc):
+        def add_bias(i, k, cc):
             if cc == 0:
-                grouped = stage.tile([P, C, PACK], BF16, tag="h_grouped", align_bytes=64)
-                h_grouped[b] = grouped
+                grouped = stage.tile([P, C, PACK], BF16, tag="h_grouped%d" % k, align_bytes=64)
+                h_grouped[(i, k)] = grouped
             cols = slice(cc * P, (cc + 1) * P)
             nc.vector.tensor_tensor(
-                out=h_grouped[b][:, cols, :],
-                in0=h_acc[(b, cc)][:].rearrange("p t c -> p c t"),
-                in1=bias_by_parity[:, b % 2, cols].unsqueeze(2).to_broadcast([P, P, PACK]),
+                out=h_grouped[(i, k)][:, cols, :],
+                in0=h_acc[(i, k, cc)][:].rearrange("p t c -> p c t"),
+                in1=bias[:, k * C + cc * P : k * C + (cc + 1) * P].unsqueeze(2).to_broadcast([P, P, PACK]),
                 op=ALU.add,
             )
 
-        def quantise_h(b):
-            codes = packed.tile([P, C], U32, tag="h_codes", align_bytes=64)
-            scales = packed.tile([P, C], U8, tag="h_scales", align_bytes=64)
+        def quantise_h(i, k):
+            codes = packed.tile([P, C], U32, tag="h_codes%d" % k, align_bytes=64)
+            scales = packed.tile([P, C], U8, tag="h_scales%d" % k, align_bytes=64)
             nc.vector.quantize_mx(
                 out=codes[:].bitcast(FP8X4),
                 scales=scales[:],
-                in_=h_grouped[b][:].rearrange("p c t -> p (c t)"),
+                in_=h_grouped[(i, k)][:].rearrange("p c t -> p (c t)"),
             )
-            h_codes[b] = codes
-            h_scales[b] = scales
+            h_codes[(i, k)] = codes
+            h_scales[(i, k)] = scales
 
-        def aggregate(b):
+        def aggregate(i, s):
             for wt in range(2):
-                cols = slice((b % 2) * J + wt * P, (b % 2) * J + (wt + 1) * P)
+                cols = slice(s * J + wt * P, s * J + (wt + 1) * P)
                 acc = psum_g2.tile([P, C], F32, tag="g2_acc")
-                nc.tensor.matmul_mx(
-                    out=acc[:],
-                    lhsT=a_codes[b // 2][:, cols].bitcast(FP8X4),
-                    lhsT_scale=a_scales[b // 2][:, cols],
-                    rhs=h_codes[b][:].bitcast(FP8X4),
-                    rhs_scale=h_scales[b][:],
-                    start=True,
-                    stop=True,
-                )
-                g2_acc[(b, wt)] = acc
+                for k, (codes, scales) in enumerate(
+                    ((a_codes[i], a_scales[i]), (spatial_codes, spatial_scales))
+                ):
+                    nc.tensor.matmul_mx(
+                        out=acc[:],
+                        lhsT=codes[:, cols].bitcast(FP8X4),
+                        lhsT_scale=scales[:, cols],
+                        rhs=h_codes[(i, k)][:].bitcast(FP8X4),
+                        rhs_scale=h_scales[(i, k)][:],
+                        start=(k == 0),
+                        stop=(k == K - 1),
+                    )
+                g2_acc[(i, s, wt)] = acc
 
-        def add_residual(b):
+        def add_residual(i, s):
             x2_tile = results.tile([P, 2, C], F32, tag="x2")
             sums = stats.tile([P, 2], F32, tag="row_sum")
             for wt in range(2):
                 nc.vector.scalar_tensor_tensor(
                     out=x2_tile[:, wt, :],
-                    in0=g2_acc[(b, wt)][:],
+                    in0=g2_acc[(i, s, wt)][:],
                     scalar=1.0,
-                    in1=res_raw[b][:, wt, :],
+                    in1=res_raw[i][:, s, wt, :],
                     op0=ALU.mult,
                     op1=ALU.add,
                     accum_out=sums[:, wt : wt + 1],
                 )
-            nc.sync.dma_start(out=out_0[b].rearrange("(t p) c -> p t c", p=P), in_=x2_tile[:])
-            x2[b] = x2_tile
-            row_sum[b] = sums
+            nc.sync.dma_start(
+                out=out_0[2 * i + s].rearrange("(m wt) c -> m wt c", wt=2), in_=x2_tile[:]
+            )
+            x2[(i, s)] = x2_tile
+            row_sum[(i, s)] = sums
 
-        def deviation(b):
+        def deviation(i, s):
             minus_mean = stats.tile([P, 2], F32, tag="neg_mean")
-            nc.scalar.activation(out=minus_mean[:], in_=row_sum[b][:], func=ACT.Copy, scale=-1.0 / C)
+            nc.scalar.activation(out=minus_mean[:], in_=row_sum[(i, s)][:], func=ACT.Copy, scale=-1.0 / C)
             squares = stats.tile([P, 2], F32, tag="squares")
             for wt in range(2):
                 unread = stats.tile([P, C], BF16, tag="unread")
                 nc.scalar.activation(
                     out=unread[:],
-                    in_=x2[b][:, wt, :],
+                    in_=x2[(i, s)][:, wt, :],
                     func=ACT.Square,
                     bias=minus_mean[:, wt : wt + 1],
                     scale=1.0,
@@ -358,43 +350,31 @@ def tile_block_attention_guide_pb_t_kernel(
             nc.scalar.activation(
                 out=deviation_tile[:], in_=squares[:], func=ACT.Sqrt, bias=eps[:], scale=1.0 / C
             )
-            neg_mean[b] = minus_mean
-            std[b] = deviation_tile
+            neg_mean[(i, s)] = minus_mean
+            std[(i, s)] = deviation_tile
 
-        def invert_deviation(b):
+        def on_vector(i, s):
+            return i == PAIRS - 1
+
+        def invert_deviation(i, s):
             inverse = stats.tile([P, 2], F32, tag="rstd")
-            nc.vector.reciprocal(out=inverse[:], in_=std[b][:])
-            rstd[b] = inverse
-            if b % VECTOR_EVERY != VECTOR_EVERY - 1:
+            nc.vector.reciprocal(out=inverse[:], in_=std[(i, s)][:])
+            rstd[(i, s)] = inverse
+            if not on_vector(i, s):
                 offset = stats.tile([P, 2], F32, tag="neg_mean_rstd")
                 nc.vector.tensor_tensor(
-                    out=offset[:], in0=neg_mean[b][:], in1=inverse[:], op=ALU.mult
+                    out=offset[:], in0=neg_mean[(i, s)][:], in1=inverse[:], op=ALU.mult
                 )
-                neg_mean_rstd[b] = offset
+                neg_mean_rstd[(i, s)] = offset
 
-        def normalise(b):
+        def normalise(i, s):
             xn = results.tile([P, 2, C], F32, tag="xn")
-            if b % VECTOR_EVERY != VECTOR_EVERY - 1:
-                for wt in range(2):
-                    nc.scalar.activation(
-                        out=xn[:, wt, :],
-                        in_=x2[b][:, wt, :],
-                        func=ACT.Identity,
-                        bias=neg_mean_rstd[b][:, wt : wt + 1],
-                        scale=rstd[b][:, wt : wt + 1],
-                    )
-                nc.gpsimd.tensor_tensor(
-                    out=xn[:], in0=xn[:], in1=gain[:].unsqueeze(1).to_broadcast([P, 2, C]), op=ALU.mult
-                )
-                nc.gpsimd.tensor_tensor(
-                    out=xn[:], in0=xn[:], in1=shift[:].unsqueeze(1).to_broadcast([P, 2, C]), op=ALU.add
-                )
-            else:
+            if on_vector(i, s):
                 for wt in range(2):
                     nc.vector.scalar_tensor_tensor(
                         out=xn[:, wt, :],
-                        in0=x2[b][:, wt, :],
-                        scalar=neg_mean[b][:, wt : wt + 1],
+                        in0=x2[(i, s)][:, wt, :],
+                        scalar=neg_mean[(i, s)][:, wt : wt + 1],
                         in1=gain[:],
                         op0=ALU.add,
                         op1=ALU.mult,
@@ -403,59 +383,90 @@ def tile_block_attention_guide_pb_t_kernel(
                     nc.vector.scalar_tensor_tensor(
                         out=xn[:, wt, :],
                         in0=xn[:, wt, :],
-                        scalar=rstd[b][:, wt : wt + 1],
+                        scalar=rstd[(i, s)][:, wt : wt + 1],
                         in1=shift[:],
                         op0=ALU.mult,
                         op1=ALU.add,
                     )
-            nc.sync.dma_start(out=out_1[b].rearrange("(t p) c -> p t c", p=P), in_=xn[:])
+            else:
+                for wt in range(2):
+                    nc.scalar.activation(
+                        out=xn[:, wt, :],
+                        in_=x2[(i, s)][:, wt, :],
+                        func=ACT.Identity,
+                        bias=neg_mean_rstd[(i, s)][:, wt : wt + 1],
+                        scale=rstd[(i, s)][:, wt : wt + 1],
+                    )
+                for wt in range(2):
+                    nc.gpsimd.tensor_tensor(out=xn[:, wt, :], in0=xn[:, wt, :], in1=gain[:], op=ALU.mult)
+                for wt in range(2):
+                    nc.gpsimd.tensor_tensor(out=xn[:, wt, :], in0=xn[:, wt, :], in1=shift[:], op=ALU.add)
+            nc.sync.dma_start(out=out_1[2 * i + s].rearrange("(m wt) c -> m wt c", wt=2), in_=xn[:])
 
-        def in_range(b):
-            return 0 <= b < B
+        def in_range(i):
+            return 0 <= i < PAIRS
 
         def step(i):
-            for cc in range(PACK):
+            if in_range(i + 2):
+                group_g1(i + 2)
+            if in_range(i + 1):
+                scale_adj(i + 1)
+            for cc in range(CHUNKS):
                 if in_range(i):
-                    add_bias(i, cc)
-                if in_range(i + 1):
-                    conv(i + 1, cc)
-            if in_range(i - 1):
-                add_residual(i - 1)
+                    add_bias(i, 0, cc)
+                    conv(i, 1, cc)
             if in_range(i - 2):
-                invert_deviation(i - 2)
+                for s in range(2):
+                    invert_deviation(i - 2, s)
+            if in_range(i - 1):
+                add_residual(i - 1, 0)
+                aggregate(i - 1, 1)
+            if in_range(i - 2):
+                normalise(i - 2, 0)
+            for cc in range(CHUNKS):
+                if in_range(i):
+                    add_bias(i, 1, cc)
+                if in_range(i + 1):
+                    conv(i + 1, 0, cc)
+            if in_range(i - 1):
+                add_residual(i - 1, 1)
+            if in_range(i - 2):
+                normalise(i - 2, 1)
+            if i == 0:
+                quantise_spatial()
             if in_range(i):
-                if i % 2 == 0:
-                    quantise_adj(i // 2)
-                quantise_h(i)
-                aggregate(i)
+                quantise_h(i, 0)
+                quantise_h(i, 1)
             if in_range(i + 2):
                 quantise_g1(i + 2)
-            if in_range(i - 1):
-                deviation(i - 1)
-            if in_range(i - 2):
-                normalise(i - 2)
+            if in_range(i + 1):
+                quantise_adj(i + 1)
+            if in_range(i):
+                aggregate(i, 0)
             if in_range(i + 3):
                 turn_g1(i + 3)
-            if in_range(i + 2) and i % 2 == 0:
-                scale_adj((i + 2) // 2)
+            if in_range(i - 1):
+                for s in range(2):
+                    deviation(i - 1, s)
 
         load_g1(0)
         load_weights()
         load_adj(0)
         load_spatial()
-        for b in range(1, B + 4):
-            if in_range(b):
-                load_g1(b)
-                if b % 2 == 0:
-                    load_adj(b // 2)
-            if in_range(b - 4):
-                load_res(b - 4)
+        load_g1(1)
+        for i in range(2, PAIRS + 2):
+            if in_range(i):
+                load_g1(i)
+            if in_range(i - 1):
+                load_adj(i - 1)
+            load_res(i - 2)
 
+        zero_other_rows()
         spread_rows()
         step(-3)
         turn_weights()
         step(-2)
         quantise_weights()
         place_spatial()
-        for i in range(-1, B + 2):
+        for i in range(-1, PAIRS + 2):
             step(i)

@@ -22,6 +22,8 @@ PAIRS = B // 2
 HALF = P // 2
 PACK = 4
 CHUNKS = C // P
+VTAIL = 1
+VUNITS = ((1, 1),)
 S2_COLS = 64
 
 FLOPS = 2 * B * J * C * (K * C) + 2 * B * (K * J) * J * C
@@ -33,10 +35,10 @@ def tile_block_attention_guide_pb_t_kernel(
     nc = tc.nc
     with ExitStack() as ctx:
         consts = ctx.enter_context(tc.tile_pool(name="consts", bufs=1))
-        inputs = ctx.enter_context(tc.tile_pool(name="inputs", bufs=1))
+        inputs = ctx.enter_context(tc.tile_pool(name="inputs", bufs=4))
         stage = ctx.enter_context(tc.tile_pool(name="stage", bufs=2))
         packed = ctx.enter_context(tc.tile_pool(name="packed", bufs=3))
-        results = ctx.enter_context(tc.tile_pool(name="results", bufs=6))
+        results = ctx.enter_context(tc.tile_pool(name="results", bufs=8))
         stats = ctx.enter_context(tc.tile_pool(name="stats", bufs=6))
         psum_turn = ctx.enter_context(tc.psum_pool(name="psum_turn", bufs=2))
         psum_h = ctx.enter_context(tc.psum_pool(name="psum_h", bufs=4))
@@ -52,10 +54,11 @@ def tile_block_attention_guide_pb_t_kernel(
         nc.vector.memset(vector_rows[:].bitcast(I32), 0)
         ones = consts.tile([P, P], BF16)
         nc.vector.memset(ones[:], 1.0)
-        nc.scalar.dma_start(out=vector_rows[0:1, 0 : 2 * C], in_=conv2_b.rearrange("(o n) -> o n", o=1))
-        nc.scalar.dma_start(out=vector_rows[0:1, 4 * C : 4 * C + 1], in_=s2.rearrange("(o n) -> o n", o=1))
-        nc.scalar.dma_start(out=vector_rows[0:1, 2 * C : 3 * C], in_=norm2_g.rearrange("(o n) -> o n", o=1))
-        nc.scalar.dma_start(out=vector_rows[0:1, 3 * C : 4 * C], in_=norm2_b.rearrange("(o n) -> o n", o=1))
+
+        def load_vector(vector, column):
+            row = vector.rearrange("(o n) -> o n", o=1)
+            nc.sync.dma_start(out=vector_rows[0:1, column : column + row.shape[1]], in_=row)
+
         first_sqrt = consts.tile([P, 1], F32)
         nc.scalar.activation(out=first_sqrt[:], in_=eps[:], func=ACT.Sqrt)
 
@@ -64,20 +67,23 @@ def tile_block_attention_guide_pb_t_kernel(
         shift = consts.tile([P, C], BF16)
         s2_f32 = consts.tile([P, 1], F32)
 
-        def spread_rows():
+        def spread_bias():
             for k in range(K):
-                spread = psum_h.tile([P, C], F32, tag="h_acc")
+                spread = psum_g2.tile([P, C], F32, tag="g2_acc")
                 nc.tensor.matmul(
                     out=spread[:], lhsT=ones[:], rhs=vector_rows[:, k * C : (k + 1) * C], start=True, stop=True
                 )
-                nc.vector.tensor_copy(out=bias[:, k * C : (k + 1) * C], in_=spread[:])
-            spread_s2 = psum_g2.tile([P, S2_COLS], F32, tag="g2_acc")
+                nc.scalar.copy(out=bias[:, k * C : (k + 1) * C], in_=spread[:])
+        def spread_s2():
+            spread = psum_g2.tile([P, S2_COLS], F32, tag="g2_acc")
             nc.tensor.matmul(
-                out=spread_s2[:], lhsT=ones[:], rhs=vector_rows[:, 4 * C :], start=True, stop=True
+                out=spread[:], lhsT=ones[:], rhs=vector_rows[:, 4 * C :], start=True, stop=True
             )
-            nc.scalar.copy(out=s2_f32[:], in_=spread_s2[:, 0:1])
+            nc.scalar.copy(out=s2_f32[:], in_=spread[:, 0:1])
+
+        def spread_norm():
             for n, spread_to in ((2, gain), (3, shift)):
-                spread = psum_h.tile([P, C], F32, tag="h_acc")
+                spread = psum_turn.tile([P, C], F32, tag="turned")
                 nc.tensor.matmul(
                     out=spread[:], lhsT=ones[:], rhs=vector_rows[:, n * C : (n + 1) * C], start=True, stop=True
                 )
@@ -90,15 +96,15 @@ def tile_block_attention_guide_pb_t_kernel(
         w_codes = consts.tile([P, K * C], U32, align_bytes=64)
         w_scales = consts.tile([P, K * C], U8, align_bytes=64)
 
-        def load_weights():
-            for n in range(W_PARTS):
+        def load_weights(parts):
+            for n in parts:
                 nc.sync.dma_start(
                     out=w_raw[:, n],
                     in_=conv2_w.rearrange("(n m p) c -> n p m c", n=W_PARTS, p=P)[n],
                 )
 
-        def turn_weights():
-            for n in range(W_PARTS):
+        def turn_weights(parts):
+            for n in parts:
                 turned_w = psum_h.tile([P, 2, 2, P], F32, tag="h_acc")
                 for m in range(2):
                     for u in range(2):
@@ -115,29 +121,41 @@ def tile_block_attention_guide_pb_t_kernel(
                 else:
                     nc.scalar.copy(out=words_out, in_=words_in)
 
-        def quantise_weights():
-            for k in range(K):
+        def quantise_weights(k):
+            if True:
                 nc.vector.quantize_mx(
                     out=w_codes[:, k * C : (k + 1) * C].bitcast(FP8X4),
                     scales=w_scales[:, k * C : (k + 1) * C],
                     in_=w_grouped[:, k * C * PACK : (k + 1) * C * PACK],
                 )
 
-        a_grouped = [
-            consts.tile([P, 2, J, PACK], BF16, name="a_grouped%d" % n, align_bytes=64) for n in range(2)
-        ]
+        A_WORDS = J + J // PACK
+        adj_packed = [consts.tile([P, A_WORDS], U32, name="adj_packed%d" % n, align_bytes=64) for n in range(2)]
+        adj_padded = [consts.tile([P, 2, A_WORDS], U32, name="adj_padded%d" % n, align_bytes=64) for n in range(2)]
+        spatial_packed = consts.tile([P, A_WORDS], U32, align_bytes=64)
+        spatial_padded = consts.tile([P, 2, A_WORDS], U32, align_bytes=64)
         spatial_raw = consts.tile([P, PACK, J], BF16)
-        spatial_grouped = consts.tile([P, 2, J, PACK], BF16, align_bytes=64)
-        spatial_codes = consts.tile([P, 2 * J], U32, align_bytes=64)
-        spatial_scales = consts.tile([P, 2 * J], U8, align_bytes=64)
+        spatial_grouped = consts.tile([P, J, PACK], BF16, align_bytes=64)
 
         def own_rows(s):
             return slice(s * HALF, (s + 1) * HALF)
 
         def zero_other_rows():
-            for tile in (spatial_grouped, a_grouped[0], a_grouped[1]):
+            for tile in (spatial_packed, adj_packed[0], adj_packed[1]):
+                nc.gpsimd.memset(tile[:, J:].bitcast(I32), 0)
+            for tile in (spatial_padded, adj_padded[0], adj_padded[1]):
                 for s in range(2):
-                    nc.gpsimd.memset(tile[own_rows(1 - s), s].rearrange("p w t -> p (w t)").bitcast(I32), 0)
+                    nc.gpsimd.memset(tile[own_rows(1 - s), s].bitcast(I32), 0)
+
+        def quantise_a(grouped, tile, padded):
+            nc.vector.quantize_mx(
+                out=tile[:, 0:J].bitcast(FP8X4),
+                scales=tile[:, J:].bitcast(U8),
+                in_=grouped[:].rearrange("p w t -> p (w t)"),
+            )
+            for s in range(2):
+                rows = own_rows(s)
+                nc.sync.dma_start(out=padded[rows, s].bitcast(I32), in_=tile[rows].bitcast(I32))
 
         def load_spatial():
             for s in range(2):
@@ -147,22 +165,9 @@ def tile_block_attention_guide_pb_t_kernel(
                 )
 
         def place_spatial():
-            for s in range(2):
-                rows = own_rows(s)
-                nc.gpsimd.tensor_scalar(
-                    out=spatial_grouped[rows, s].rearrange("p (wt m) t -> p wt m t", wt=2),
-                    in0=spatial_raw[rows].rearrange("p t (m wt) -> p wt m t", wt=2),
-                    scalar1=1.0,
-                    scalar2=0.0,
-                    op0=ALU.mult,
-                    op1=ALU.add,
-                )
-
-        def quantise_spatial():
-            nc.vector.quantize_mx(
-                out=spatial_codes[:].bitcast(FP8X4),
-                scales=spatial_scales[:],
-                in_=spatial_grouped[:].rearrange("p s w t -> p (s w t)"),
+            nc.scalar.copy(
+                out=spatial_grouped[:].rearrange("p (wt m) t -> p wt m t", wt=2),
+                in_=spatial_raw[:].rearrange("p t (m wt) -> p wt m t", wt=2),
             )
 
         g1_raw = {}
@@ -172,8 +177,7 @@ def tile_block_attention_guide_pb_t_kernel(
         g1_grouped = {}
         g1_codes = {}
         g1_scales = {}
-        a_codes = {}
-        a_scales = {}
+        adj_grouped = {}
         h_acc = {}
         h_grouped = {}
         h_codes = {}
@@ -182,51 +186,51 @@ def tile_block_attention_guide_pb_t_kernel(
         x2 = {}
         row_sum = {}
         neg_mean = {}
+        squares = {}
         std = {}
         rstd = {}
-        neg_mean_rstd = {}
+        offset = {}
+        xn_tile = {}
 
         def load_g1(i):
-            g1_raw[i] = inputs.tile([P, PACK, C], BF16, name="g1_raw%d" % i)
+            g1_raw[i] = inputs.tile([P, PACK, C], BF16, tag="g1_raw", name="g1_raw%d" % i)
             nc.sync.dma_start(
                 out=g1_raw[i][:], in_=g1[2 * i : 2 * i + 2].rearrange("b (r t) c -> (b r) t c", t=PACK)
             )
 
         def load_adj(i):
-            adj_raw[i] = inputs.tile([P, PACK, J], BF16, name="adj_raw%d" % i)
+            adj_raw[i] = inputs.tile([P, PACK, J], BF16, tag="adj_raw", name="adj_raw%d" % i)
             nc.sync.dma_start(
                 out=adj_raw[i][:], in_=adj[2 * i : 2 * i + 2, 0].rearrange("b (r t) w -> (b r) t w", t=PACK)
             )
 
         def load_res(i):
-            res_raw[i] = inputs.tile([P, 2, 2, C], BF16, name="res_raw%d" % i)
+            res_raw[i] = inputs.tile([P, 2, 2, C], BF16, tag="res_raw", name="res_raw%d" % i)
             for s in range(2):
                 nc.sync.dma_start(
                     out=res_raw[i][:, s], in_=res1[2 * i + s].rearrange("(m wt) c -> m wt c", wt=2)
                 )
 
-        def turn_g1(i):
-            g1_turned[i] = []
-            for half in range(2):
-                turned = psum_turn.tile([P, 2, 2, P], F32, tag="turned")
-                for t in range(2):
-                    for u in range(2):
-                        nc.tensor.transpose(
-                            turned[:, t, u, :],
-                            g1_raw[i][:, 2 * half + t, :].bitcast(F32)[:, u : 2 * P : 2],
-                            identity[:],
-                        )
-                g1_turned[i].append(turned)
+        def turn_g1(i, half):
+            turned = psum_turn.tile([P, 2, 2, P], F32, tag="turned")
+            for t in range(2):
+                for u in range(2):
+                    nc.tensor.transpose(
+                        turned[:, t, u, :],
+                        g1_raw[i][:, 2 * half + t, :].bitcast(F32)[:, u : 2 * P : 2],
+                        identity[:],
+                    )
+            g1_turned[(i, half)] = turned
 
-        def group_g1(i):
-            grouped = stage.tile([P, PACK * P * PACK], BF16, tag="g1_grouped", align_bytes=64)
-            for half in range(2):
-                cols = slice(half * 2 * P * PACK, (half + 1) * 2 * P * PACK)
-                nc.scalar.copy(
-                    out=grouped[:, cols].bitcast(F32).rearrange("q (t n u) -> q t n u", t=2, u=2),
-                    in_=g1_turned[i][half][:].rearrange("q t u n -> q t n u"),
-                )
-            g1_grouped[i] = grouped
+        def group_g1(i, half):
+            if half == 0:
+                grouped = stage.tile([P, PACK * P * PACK], BF16, tag="g1_grouped", align_bytes=64)
+                g1_grouped[i] = grouped
+            cols = slice(half * 2 * P * PACK, (half + 1) * 2 * P * PACK)
+            nc.scalar.copy(
+                out=g1_grouped[i][:, cols].bitcast(F32).rearrange("q (t n u) -> q t n u", t=2, u=2),
+                in_=g1_turned[(i, half)][:].rearrange("q t u n -> q t n u"),
+            )
 
         def quantise_g1(i):
             codes = packed.tile([P, PACK * P], U32, tag="g1_codes", align_bytes=64)
@@ -236,25 +240,14 @@ def tile_block_attention_guide_pb_t_kernel(
             g1_scales[i] = scales
 
         def scale_adj(i):
-            for s in range(2):
-                rows = own_rows(s)
-                nc.scalar.activation(
-                    out=a_grouped[i % 2][rows, s].rearrange("p (wt m) t -> p wt m t", wt=2),
-                    in_=adj_raw[i][rows].rearrange("p t (m wt) -> p wt m t", wt=2),
-                    func=ACT.Copy,
-                    scale=s2_f32[rows, :],
-                )
-
-        def quantise_adj(i):
-            codes = packed.tile([P, 2 * J], U32, tag="a_codes", align_bytes=64)
-            scales = packed.tile([P, 2 * J], U8, tag="a_scales", align_bytes=64)
-            nc.vector.quantize_mx(
-                out=codes[:].bitcast(FP8X4),
-                scales=scales[:],
-                in_=a_grouped[i % 2][:].rearrange("p s w t -> p (s w t)"),
+            grouped = stage.tile([P, J, PACK], BF16, tag="adj_grouped", align_bytes=64)
+            nc.scalar.activation(
+                out=grouped[:].rearrange("p (wt m) t -> p wt m t", wt=2),
+                in_=adj_raw[i][:].rearrange("p t (m wt) -> p wt m t", wt=2),
+                func=ACT.Copy,
+                scale=s2_f32[:],
             )
-            a_codes[i] = codes
-            a_scales[i] = scales
+            adj_grouped[i] = grouped
 
         def conv(i, k, cc):
             acc = psum_h.tile([P, PACK, P], F32, tag="h_acc")
@@ -297,15 +290,13 @@ def tile_block_attention_guide_pb_t_kernel(
 
         def aggregate(i, s):
             for wt in range(2):
-                cols = slice(s * J + wt * P, s * J + (wt + 1) * P)
+                cols = slice(wt * P, (wt + 1) * P)
                 acc = psum_g2.tile([P, C], F32, tag="g2_acc")
-                for k, (codes, scales) in enumerate(
-                    ((a_codes[i], a_scales[i]), (spatial_codes, spatial_scales))
-                ):
+                for k, padded in enumerate((adj_padded[i % 2], spatial_padded)):
                     nc.tensor.matmul_mx(
                         out=acc[:],
-                        lhsT=codes[:, cols].bitcast(FP8X4),
-                        lhsT_scale=scales[:, cols],
+                        lhsT=padded[:, s, cols].bitcast(FP8X4),
+                        lhsT_scale=padded[:, s, J:].bitcast(U8)[:, cols],
                         rhs=h_codes[(i, k)][:].bitcast(FP8X4),
                         rhs_scale=h_scales[(i, k)][:],
                         start=(k == 0),
@@ -315,7 +306,9 @@ def tile_block_attention_guide_pb_t_kernel(
 
         def add_residual(i, s):
             x2_tile = results.tile([P, 2, C], F32, tag="x2")
-            sums = stats.tile([P, 2], F32, tag="row_sum")
+            if s == 0:
+                sums = stats.tile([P, 2, 2], F32, tag="row_sum")
+                row_sum[i] = sums
             for wt in range(2):
                 nc.vector.scalar_tensor_tensor(
                     out=x2_tile[:, wt, :],
@@ -324,149 +317,216 @@ def tile_block_attention_guide_pb_t_kernel(
                     in1=res_raw[i][:, s, wt, :],
                     op0=ALU.mult,
                     op1=ALU.add,
-                    accum_out=sums[:, wt : wt + 1],
+                    accum_out=row_sum[i][:, s, wt : wt + 1],
                 )
             nc.sync.dma_start(
                 out=out_0[2 * i + s].rearrange("(m wt) c -> m wt c", wt=2), in_=x2_tile[:]
             )
             x2[(i, s)] = x2_tile
-            row_sum[(i, s)] = sums
 
-        def deviation(i, s):
-            minus_mean = stats.tile([P, 2], F32, tag="neg_mean")
-            nc.scalar.activation(out=minus_mean[:], in_=row_sum[(i, s)][:], func=ACT.Copy, scale=-1.0 / C)
-            squares = stats.tile([P, 2], F32, tag="squares")
+        def negate_mean(i):
+            minus_mean = stats.tile([P, 2, 2], F32, tag="neg_mean")
+            nc.scalar.activation(out=minus_mean[:], in_=row_sum[i][:], func=ACT.Copy, scale=-1.0 / C)
+            neg_mean[i] = minus_mean
+
+        def square(i, s):
+            if s == 0:
+                sums = stats.tile([P, 2, 2], F32, tag="squares")
+                squares[i] = sums
             for wt in range(2):
                 unread = stats.tile([P, C], BF16, tag="unread")
                 nc.scalar.activation(
                     out=unread[:],
                     in_=x2[(i, s)][:, wt, :],
                     func=ACT.Square,
-                    bias=minus_mean[:, wt : wt + 1],
+                    bias=neg_mean[i][:, s, wt : wt + 1],
                     scale=1.0,
-                    accum_out=squares[:, wt : wt + 1],
+                    accum_out=squares[i][:, s, wt : wt + 1],
                 )
-            deviation_tile = stats.tile([P, 2], F32, tag="std")
-            nc.scalar.activation(
-                out=deviation_tile[:], in_=squares[:], func=ACT.Sqrt, bias=eps[:], scale=1.0 / C
+
+        def root(i):
+            deviation = stats.tile([P, 2, 2], F32, tag="std")
+            nc.scalar.activation(out=deviation[:], in_=squares[i][:], func=ACT.Sqrt, bias=eps[:], scale=1.0 / C)
+            std[i] = deviation
+
+        def invert(i):
+            inverse = stats.tile([P, 2, 2], F32, tag="rstd")
+            nc.vector.reciprocal(out=inverse[:], in_=std[i][:])
+            rstd[i] = inverse
+
+        def offset_mean(i):
+            product = stats.tile([P, 2, 2], F32, tag="offset")
+            nc.vector.tensor_tensor(out=product[:], in0=neg_mean[i][:], in1=rstd[i][:], op=ALU.mult)
+            offset[i] = product
+
+        def on_vector(i, s, wt):
+            return i >= PAIRS - VTAIL or (s, wt) in VUNITS
+
+        def xn_of(i, s):
+            if (i, s) not in xn_tile:
+                xn = results.tile([P, 2, C], F32, tag="xn")
+                xn_tile[(i, s)] = xn
+            return xn_tile[(i, s)]
+
+        def vector_times_gain(i, s, wt):
+            nc.vector.scalar_tensor_tensor(
+                out=xn_of(i, s)[:, wt, :],
+                in0=x2[(i, s)][:, wt, :],
+                scalar=neg_mean[i][:, s, wt : wt + 1],
+                in1=gain[:],
+                op0=ALU.add,
+                op1=ALU.mult,
             )
-            neg_mean[(i, s)] = minus_mean
-            std[(i, s)] = deviation_tile
 
-        def on_vector(i, s):
-            return i == PAIRS - 1
+        def vector_plus_shift(i, s, wt):
+            nc.vector.scalar_tensor_tensor(
+                out=xn_of(i, s)[:, wt, :],
+                in0=xn_of(i, s)[:, wt, :],
+                scalar=rstd[i][:, s, wt : wt + 1],
+                in1=shift[:],
+                op0=ALU.mult,
+                op1=ALU.add,
+            )
 
-        def invert_deviation(i, s):
-            inverse = stats.tile([P, 2], F32, tag="rstd")
-            nc.vector.reciprocal(out=inverse[:], in_=std[(i, s)][:])
-            rstd[(i, s)] = inverse
-            if not on_vector(i, s):
-                offset = stats.tile([P, 2], F32, tag="neg_mean_rstd")
-                nc.vector.tensor_tensor(
-                    out=offset[:], in0=neg_mean[(i, s)][:], in1=inverse[:], op=ALU.mult
-                )
-                neg_mean_rstd[(i, s)] = offset
+        def standardise(i, s, wt):
+            nc.scalar.activation(
+                out=xn_of(i, s)[:, wt, :],
+                in_=x2[(i, s)][:, wt, :],
+                func=ACT.Identity,
+                bias=offset[i][:, s, wt : wt + 1],
+                scale=rstd[i][:, s, wt : wt + 1],
+            )
 
-        def normalise(i, s):
-            xn = results.tile([P, 2, C], F32, tag="xn")
-            if on_vector(i, s):
-                for wt in range(2):
-                    nc.vector.scalar_tensor_tensor(
-                        out=xn[:, wt, :],
-                        in0=x2[(i, s)][:, wt, :],
-                        scalar=neg_mean[(i, s)][:, wt : wt + 1],
-                        in1=gain[:],
-                        op0=ALU.add,
-                        op1=ALU.mult,
-                    )
-                for wt in range(2):
-                    nc.vector.scalar_tensor_tensor(
-                        out=xn[:, wt, :],
-                        in0=xn[:, wt, :],
-                        scalar=rstd[(i, s)][:, wt : wt + 1],
-                        in1=shift[:],
-                        op0=ALU.mult,
-                        op1=ALU.add,
-                    )
-            else:
-                for wt in range(2):
-                    nc.scalar.activation(
-                        out=xn[:, wt, :],
-                        in_=x2[(i, s)][:, wt, :],
-                        func=ACT.Identity,
-                        bias=neg_mean_rstd[(i, s)][:, wt : wt + 1],
-                        scale=rstd[(i, s)][:, wt : wt + 1],
-                    )
-                for wt in range(2):
-                    nc.gpsimd.tensor_tensor(out=xn[:, wt, :], in0=xn[:, wt, :], in1=gain[:], op=ALU.mult)
-                for wt in range(2):
-                    nc.gpsimd.tensor_tensor(out=xn[:, wt, :], in0=xn[:, wt, :], in1=shift[:], op=ALU.add)
-            nc.sync.dma_start(out=out_1[2 * i + s].rearrange("(m wt) c -> m wt c", wt=2), in_=xn[:])
+        def gpsimd_unit(i, s, wt):
+            xn = xn_of(i, s)
+            nc.gpsimd.tensor_tensor(out=xn[:, wt, :], in0=xn[:, wt, :], in1=gain[:], op=ALU.mult)
+            nc.gpsimd.tensor_tensor(out=xn[:, wt, :], in0=xn[:, wt, :], in1=shift[:], op=ALU.add)
+
+        def store_xn(i, s):
+            nc.sync.dma_start(out=out_1[2 * i + s].rearrange("(m wt) c -> m wt c", wt=2), in_=xn_of(i, s)[:])
+
+        UNITS = [(s, wt) for s in range(2) for wt in range(2)]
 
         def in_range(i):
             return 0 <= i < PAIRS
 
         def step(i):
-            if in_range(i + 2):
-                group_g1(i + 2)
-            if in_range(i + 1):
-                scale_adj(i + 1)
-            for cc in range(CHUNKS):
-                if in_range(i):
-                    add_bias(i, 0, cc)
-                    conv(i, 1, cc)
-            if in_range(i - 2):
-                for s in range(2):
-                    invert_deviation(i - 2, s)
-            if in_range(i - 1):
-                add_residual(i - 1, 0)
-                aggregate(i - 1, 1)
-            if in_range(i - 2):
-                normalise(i - 2, 0)
-            for cc in range(CHUNKS):
-                if in_range(i):
-                    add_bias(i, 1, cc)
+            now, before, next_one = (in_range(i), in_range(i - 1), in_range(i + 1))
+            if i >= 0:
+                if in_range(i + 3):
+                    load_g1(i + 3)
+                if in_range(i + 2):
+                    load_adj(i + 2)
                 if in_range(i + 1):
-                    conv(i + 1, 0, cc)
-            if in_range(i - 1):
-                add_residual(i - 1, 1)
+                    load_res(i + 1)
             if in_range(i - 2):
-                normalise(i - 2, 1)
-            if i == 0:
-                quantise_spatial()
-            if in_range(i):
+                for s, wt in UNITS:
+                    if not on_vector(i - 2, s, wt):
+                        standardise(i - 2, s, wt)
+                for s in range(2):
+                    for wt in range(2):
+                        if not on_vector(i - 2, s, wt):
+                            gpsimd_unit(i - 2, s, wt)
+                    if not on_vector(i - 2, s, 0):
+                        store_xn(i - 2, s)
+            for n in range(K * CHUNKS):
+                k, cc = divmod(n, CHUNKS)
+                if now:
+                    add_bias(i, k, cc)
+                    if k == 0:
+                        conv(i, 1, cc)
+                if k == 1 and next_one:
+                    conv(i + 1, 0, cc)
+                if n == 1 and before:
+                    add_residual(i - 1, 0)
+                    aggregate(i - 1, 1)
+                if n == 3 and i == 0:
+                    quantise_g1(1)
+                    turn_g1(2, 0)
+                    turn_g1(2, 1)
+                    group_g1(2, 0)
+                    group_g1(2, 1)
+                if n == 5 and i == 0:
+                    spread_norm()
+                if n == 6 and i == 0:
+                    quantise_a(spatial_grouped, spatial_packed, spatial_padded)
+                    quantise_a(adj_grouped[0], adj_packed[0], adj_padded[0])
+                if n == 1 and i > 0 and in_range(i + 2):
+                    group_g1(i + 2, 0)
+                    group_g1(i + 2, 1)
+                if n == 2 and next_one:
+                    scale_adj(i + 1)
+                if n == 3 and before:
+                    add_residual(i - 1, 1)
+                    negate_mean(i - 1)
+                    square(i - 1, 0)
+                    square(i - 1, 1)
+                    root(i - 1)
+            last = i == PAIRS - 1
+            if last:
                 quantise_h(i, 0)
                 quantise_h(i, 1)
+                aggregate(i, 0)
             if in_range(i + 2):
                 quantise_g1(i + 2)
-            if in_range(i + 1):
-                quantise_adj(i + 1)
-            if in_range(i):
+            if next_one:
+                quantise_a(adj_grouped[i + 1], adj_packed[(i + 1) % 2], adj_padded[(i + 1) % 2])
+            if before:
+                invert(i - 1)
+            if now and not last:
+                quantise_h(i, 0)
+            if before:
+                for s, wt in UNITS:
+                    if on_vector(i - 1, s, wt):
+                        vector_times_gain(i - 1, s, wt)
+            if now and not last:
+                quantise_h(i, 1)
                 aggregate(i, 0)
-            if in_range(i + 3):
-                turn_g1(i + 3)
-            if in_range(i - 1):
+            if before:
                 for s in range(2):
-                    deviation(i - 1, s)
+                    for wt in range(2):
+                        if on_vector(i - 1, s, wt):
+                            vector_plus_shift(i - 1, s, wt)
+                    if on_vector(i - 1, s, 0):
+                        store_xn(i - 1, s)
+                offset_mean(i - 1)
+            if in_range(i + 3):
+                turn_g1(i + 3, 0)
+                turn_g1(i + 3, 1)
 
         load_g1(0)
-        load_weights()
+        load_weights((0, 1))
+        load_vector(conv2_b, 0)
+        load_vector(s2, 4 * C)
+        load_weights((2, 3))
         load_adj(0)
         load_spatial()
         load_g1(1)
-        for i in range(2, PAIRS + 2):
-            if in_range(i):
-                load_g1(i)
-            if in_range(i - 1):
-                load_adj(i - 1)
-            load_res(i - 2)
+        load_vector(norm2_g, 2 * C)
+        load_vector(norm2_b, 3 * C)
+        load_res(0)
+        load_g1(2)
+        load_adj(1)
 
         zero_other_rows()
-        spread_rows()
-        step(-3)
-        turn_weights()
-        step(-2)
-        quantise_weights()
+        turn_g1(0, 0)
+        turn_g1(0, 1)
+        group_g1(0, 0)
+        group_g1(0, 1)
+        turn_weights((0, 1))
+        quantise_g1(0)
+        spread_bias()
+        turn_weights((2, 3))
+        quantise_weights(0)
+        quantise_weights(1)
+        spread_s2()
+        turn_g1(1, 0)
+        turn_g1(1, 1)
+        group_g1(1, 0)
+        group_g1(1, 1)
+        for cc in range(CHUNKS):
+            conv(0, 0, cc)
+        scale_adj(0)
         place_spatial()
-        for i in range(-1, PAIRS + 2):
+        for i in range(0, PAIRS + 2):
             step(i)

@@ -22,8 +22,6 @@ PAIRS = B // 2
 HALF = P // 2
 PACK = 4
 CHUNKS = C // P
-VTAIL = 1
-VUNITS = ((1, 1),)
 S2_COLS = 64
 
 FLOPS = 2 * B * J * C * (K * C) + 2 * B * (K * J) * J * C
@@ -66,6 +64,7 @@ def tile_block_attention_guide_pb_t_kernel(
         gain = consts.tile([P, C], BF16)
         shift = consts.tile([P, C], BF16)
         s2_f32 = consts.tile([P, 1], F32)
+        columns = consts.tile([P, 2 * CHUNKS], F32)
 
         def spread_bias():
             for k in range(K):
@@ -82,6 +81,16 @@ def tile_block_attention_guide_pb_t_kernel(
             nc.scalar.copy(out=s2_f32[:], in_=spread[:, 0:1])
 
         def spread_norm():
+            spread = psum_turn.tile([P, 2 * CHUNKS, S2_COLS], F32, tag="turned")
+            for n in range(2 * CHUNKS):
+                nc.tensor.matmul(
+                    out=spread[:, n, :],
+                    lhsT=vector_rows[:, 2 * C + n * P : 2 * C + (n + 1) * P],
+                    rhs=ones[:, 0:S2_COLS],
+                    start=True,
+                    stop=True,
+                )
+            nc.scalar.copy(out=columns[:], in_=spread[:, :, 0])
             for n, spread_to in ((2, gain), (3, shift)):
                 spread = psum_turn.tile([P, C], F32, tag="turned")
                 nc.tensor.matmul(
@@ -190,6 +199,7 @@ def tile_block_attention_guide_pb_t_kernel(
         std = {}
         rstd = {}
         offset = {}
+        scaled_xn = {}
         xn_tile = {}
 
         def load_g1(i):
@@ -324,13 +334,16 @@ def tile_block_attention_guide_pb_t_kernel(
             )
             x2[(i, s)] = x2_tile
 
-        def negate_mean(i):
-            minus_mean = stats.tile([P, 2, 2], F32, tag="neg_mean")
-            nc.scalar.activation(out=minus_mean[:], in_=row_sum[i][:], func=ACT.Copy, scale=-1.0 / C)
-            neg_mean[i] = minus_mean
+        BOTH = slice(0, 2)
+
+        def negate_mean(i, s=BOTH):
+            if i not in neg_mean:
+                minus_mean = stats.tile([P, 2, 2], F32, tag="neg_mean")
+                neg_mean[i] = minus_mean
+            nc.scalar.activation(out=neg_mean[i][:, s, :], in_=row_sum[i][:, s, :], func=ACT.Copy, scale=-1.0 / C)
 
         def square(i, s):
-            if s == 0:
+            if i not in squares:
                 sums = stats.tile([P, 2, 2], F32, tag="squares")
                 squares[i] = sums
             for wt in range(2):
@@ -344,23 +357,24 @@ def tile_block_attention_guide_pb_t_kernel(
                     accum_out=squares[i][:, s, wt : wt + 1],
                 )
 
-        def root(i):
-            deviation = stats.tile([P, 2, 2], F32, tag="std")
-            nc.scalar.activation(out=deviation[:], in_=squares[i][:], func=ACT.Sqrt, bias=eps[:], scale=1.0 / C)
-            std[i] = deviation
+        def root(i, s=BOTH):
+            if i not in std:
+                deviation = stats.tile([P, 2, 2], F32, tag="std")
+                std[i] = deviation
+            nc.scalar.activation(
+                out=std[i][:, s, :], in_=squares[i][:, s, :], func=ACT.Sqrt, bias=eps[:], scale=1.0 / C
+            )
 
-        def invert(i):
-            inverse = stats.tile([P, 2, 2], F32, tag="rstd")
-            nc.vector.reciprocal(out=inverse[:], in_=std[i][:])
-            rstd[i] = inverse
+        def invert(i, s=BOTH):
+            if i not in rstd:
+                inverse = stats.tile([P, 2, 2], F32, tag="rstd")
+                rstd[i] = inverse
+            nc.vector.reciprocal(out=rstd[i][:, s, :], in_=std[i][:, s, :])
 
         def offset_mean(i):
             product = stats.tile([P, 2, 2], F32, tag="offset")
             nc.vector.tensor_tensor(out=product[:], in0=neg_mean[i][:], in1=rstd[i][:], op=ALU.mult)
             offset[i] = product
-
-        def on_vector(i, s, wt):
-            return i >= PAIRS - VTAIL or (s, wt) in VUNITS
 
         def xn_of(i, s):
             if (i, s) not in xn_tile:
@@ -397,6 +411,27 @@ def tile_block_attention_guide_pb_t_kernel(
                 scale=rstd[i][:, s, wt : wt + 1],
             )
 
+        def turn_forth(i, s, wt):
+            turned = psum_turn.tile([P, CHUNKS, P], F32, tag="turned")
+            for cc in range(CHUNKS):
+                nc.tensor.transpose(turned[:, cc, :], xn_of(i, s)[:, wt, cc * P : (cc + 1) * P], identity[:])
+            scaled = stage.tile([P, CHUNKS, P], F32, tag="scaled")
+            for cc in range(CHUNKS):
+                nc.scalar.activation(
+                    out=scaled[:, cc, :],
+                    in_=turned[:, cc, :],
+                    func=ACT.Identity,
+                    bias=columns[:, CHUNKS + cc : CHUNKS + cc + 1],
+                    scale=columns[:, cc : cc + 1],
+                )
+            scaled_xn[(i, s, wt)] = scaled
+
+        def turn_back(i, s, wt):
+            turned = psum_turn.tile([P, CHUNKS, P], F32, tag="turned")
+            for cc in range(CHUNKS):
+                nc.tensor.transpose(turned[:, cc, :], scaled_xn[(i, s, wt)][:, cc, :], identity[:])
+            nc.scalar.copy(out=xn_of(i, s)[:, wt, :], in_=turned[:].rearrange("p c n -> p (c n)"))
+
         def gpsimd_unit(i, s, wt):
             xn = xn_of(i, s)
             nc.gpsimd.tensor_tensor(out=xn[:, wt, :], in0=xn[:, wt, :], in1=gain[:], op=ALU.mult)
@@ -405,37 +440,30 @@ def tile_block_attention_guide_pb_t_kernel(
         def store_xn(i, s):
             nc.sync.dma_start(out=out_1[2 * i + s].rearrange("(m wt) c -> m wt c", wt=2), in_=xn_of(i, s)[:])
 
-        UNITS = [(s, wt) for s in range(2) for wt in range(2)]
-
         def in_range(i):
             return 0 <= i < PAIRS
 
         def step(i):
-            now, before, next_one = (in_range(i), in_range(i - 1), in_range(i + 1))
-            if i >= 0:
-                if in_range(i + 3):
-                    load_g1(i + 3)
-                if in_range(i + 2):
-                    load_adj(i + 2)
-                if in_range(i + 1):
-                    load_res(i + 1)
-            if in_range(i - 2):
-                for s, wt in UNITS:
-                    if not on_vector(i - 2, s, wt):
-                        standardise(i - 2, s, wt)
-                for s in range(2):
-                    for wt in range(2):
-                        if not on_vector(i - 2, s, wt):
-                            gpsimd_unit(i - 2, s, wt)
-                    if not on_vector(i - 2, s, 0):
-                        store_xn(i - 2, s)
+            before, next_one = (in_range(i - 1), in_range(i + 1))
+            done = i - 2
+            if in_range(i + 3):
+                load_g1(i + 3)
+            if in_range(i + 2):
+                load_adj(i + 2)
+            if in_range(i + 1):
+                load_res(i + 1)
+            if in_range(done):
+                for s, wt in ((0, 0), (0, 1), (1, 0), (1, 1)):
+                    standardise(done, s, wt)
+                for s, wt in ((0, 0), (0, 1), (1, 0)):
+                    gpsimd_unit(done, s, wt)
+                store_xn(done, 0)
             for n in range(K * CHUNKS):
                 k, cc = divmod(n, CHUNKS)
-                if now:
-                    add_bias(i, k, cc)
-                    if k == 0:
-                        conv(i, 1, cc)
-                if k == 1 and next_one:
+                add_bias(i, k, cc)
+                if k == 0:
+                    conv(i, 1, cc)
+                elif next_one:
                     conv(i + 1, 0, cc)
                 if n == 1 and before:
                     add_residual(i - 1, 0)
@@ -456,43 +484,63 @@ def tile_block_attention_guide_pb_t_kernel(
                     group_g1(i + 2, 1)
                 if n == 2 and next_one:
                     scale_adj(i + 1)
+                if n == 2 and in_range(done):
+                    turn_forth(done, 1, 1)
                 if n == 3 and before:
                     add_residual(i - 1, 1)
                     negate_mean(i - 1)
                     square(i - 1, 0)
                     square(i - 1, 1)
                     root(i - 1)
-            last = i == PAIRS - 1
-            if last:
-                quantise_h(i, 0)
-                quantise_h(i, 1)
-                aggregate(i, 0)
+                if n == 5 and in_range(done):
+                    turn_back(done, 1, 1)
+                    store_xn(done, 1)
             if in_range(i + 2):
                 quantise_g1(i + 2)
             if next_one:
                 quantise_a(adj_grouped[i + 1], adj_packed[(i + 1) % 2], adj_padded[(i + 1) % 2])
+            quantise_h(i, 0)
             if before:
                 invert(i - 1)
-            if now and not last:
-                quantise_h(i, 0)
+            quantise_h(i, 1)
+            aggregate(i, 0)
             if before:
-                for s, wt in UNITS:
-                    if on_vector(i - 1, s, wt):
-                        vector_times_gain(i - 1, s, wt)
-            if now and not last:
-                quantise_h(i, 1)
-                aggregate(i, 0)
-            if before:
-                for s in range(2):
-                    for wt in range(2):
-                        if on_vector(i - 1, s, wt):
-                            vector_plus_shift(i - 1, s, wt)
-                    if on_vector(i - 1, s, 0):
-                        store_xn(i - 1, s)
                 offset_mean(i - 1)
             if in_range(i + 3):
                 turn_g1(i + 3, 0)
                 turn_g1(i + 3, 1)
+
+        def finish():
+            last = PAIRS - 1
+            done = last - 1
+            for s, wt in ((0, 0), (0, 1)):
+                standardise(done, s, wt)
+                gpsimd_unit(done, s, wt)
+            store_xn(done, 0)
+            add_residual(last, 0)
+            aggregate(last, 1)
+            negate_mean(last, 0)
+            square(last, 0)
+            root(last, 0)
+            add_residual(last, 1)
+            negate_mean(last, 1)
+            square(last, 1)
+            root(last, 1)
+            standardise(done, 1, 1)
+            turn_forth(done, 1, 1)
+            turn_back(done, 1, 1)
+            vector_times_gain(done, 1, 0)
+            invert(last, 0)
+            vector_plus_shift(done, 1, 0)
+            store_xn(done, 1)
+            for s in range(2):
+                for wt in range(2):
+                    vector_times_gain(last, s, wt)
+                if s == 0:
+                    invert(last, 1)
+                for wt in range(2):
+                    vector_plus_shift(last, s, wt)
+                store_xn(last, s)
 
         load_g1(0)
         load_weights((0, 1))
@@ -528,5 +576,6 @@ def tile_block_attention_guide_pb_t_kernel(
             conv(0, 0, cc)
         scale_adj(0)
         place_spatial()
-        for i in range(0, PAIRS + 2):
+        for i in range(PAIRS):
             step(i)
+        finish()

@@ -432,10 +432,12 @@ def tile_block_attention_guide_pb_t_kernel(
                 nc.tensor.transpose(turned[:, cc, :], scaled_xn[(i, s, wt)][:, cc, :], identity[:])
             nc.scalar.copy(out=xn_of(i, s)[:, wt, :], in_=turned[:].rearrange("p c n -> p (c n)"))
 
-        def gpsimd_unit(i, s, wt):
-            xn = xn_of(i, s)
-            nc.gpsimd.tensor_tensor(out=xn[:, wt, :], in0=xn[:, wt, :], in1=gain[:], op=ALU.mult)
-            nc.gpsimd.tensor_tensor(out=xn[:, wt, :], in0=xn[:, wt, :], in1=shift[:], op=ALU.add)
+        def gpsimd_apply(i, s, wts, vector, op):
+            part = xn_of(i, s)[:, wts, :]
+            many = wts.stop - wts.start
+            nc.gpsimd.tensor_tensor(
+                out=part, in0=part, in1=vector[:].unsqueeze(1).to_broadcast([P, many, C]), op=op
+            )
 
         def store_xn(i, s):
             nc.sync.dma_start(out=out_1[2 * i + s].rearrange("(m wt) c -> m wt c", wt=2), in_=xn_of(i, s)[:])
@@ -455,8 +457,9 @@ def tile_block_attention_guide_pb_t_kernel(
             if in_range(done):
                 for s, wt in ((0, 0), (0, 1), (1, 0), (1, 1)):
                     standardise(done, s, wt)
-                for s, wt in ((0, 0), (0, 1), (1, 0)):
-                    gpsimd_unit(done, s, wt)
+                for vector, op in ((gain, ALU.mult), (shift, ALU.add)):
+                    gpsimd_apply(done, 0, slice(0, 2), vector, op)
+                    gpsimd_apply(done, 1, slice(0, 1), vector, op)
                 store_xn(done, 0)
             for n in range(K * CHUNKS):
                 k, cc = divmod(n, CHUNKS)
@@ -513,9 +516,12 @@ def tile_block_attention_guide_pb_t_kernel(
         def finish():
             last = PAIRS - 1
             done = last - 1
-            for s, wt in ((0, 0), (0, 1)):
-                standardise(done, s, wt)
-                gpsimd_unit(done, s, wt)
+            for wt in range(2):
+                standardise(done, 0, wt)
+            for wt in range(2):
+                gpsimd_apply(done, 0, slice(wt, wt + 1), gain, ALU.mult)
+            for wt in range(2):
+                gpsimd_apply(done, 0, slice(wt, wt + 1), shift, ALU.add)
             store_xn(done, 0)
             add_residual(last, 0)
             aggregate(last, 1)

@@ -50,7 +50,7 @@ def tile_block_attention_guide_pb_t_kernel(
 
         vector_rows = consts.tile([P, 4 * C + S2_COLS], BF16)
         nc.vector.memset(vector_rows[:].bitcast(I32), 0)
-        ones = consts.tile([P, P], BF16)
+        ones = consts.tile([P, C], BF16)
         nc.vector.memset(ones[:], 1.0)
 
         def load_vector(vector, column):
@@ -66,17 +66,22 @@ def tile_block_attention_guide_pb_t_kernel(
         s2_f32 = consts.tile([P, 1], F32)
         columns = consts.tile([P, 2 * CHUNKS], F32)
 
+        def keep_warm(times):
+            idle = psum_g2.tile([P, C], F32, tag="g2_acc")
+            for n in range(times):
+                nc.tensor.matmul(out=idle[:], lhsT=ones[:, 0:P], rhs=ones[:], start=True, stop=True)
+
         def spread_bias():
             for k in range(K):
                 spread = psum_g2.tile([P, C], F32, tag="g2_acc")
                 nc.tensor.matmul(
-                    out=spread[:], lhsT=ones[:], rhs=vector_rows[:, k * C : (k + 1) * C], start=True, stop=True
+                    out=spread[:], lhsT=ones[:, 0:P], rhs=vector_rows[:, k * C : (k + 1) * C], start=True, stop=True
                 )
                 nc.scalar.copy(out=bias[:, k * C : (k + 1) * C], in_=spread[:])
         def spread_s2():
             spread = psum_g2.tile([P, S2_COLS], F32, tag="g2_acc")
             nc.tensor.matmul(
-                out=spread[:], lhsT=ones[:], rhs=vector_rows[:, 4 * C :], start=True, stop=True
+                out=spread[:], lhsT=ones[:, 0:P], rhs=vector_rows[:, 4 * C :], start=True, stop=True
             )
             nc.scalar.copy(out=s2_f32[:], in_=spread[:, 0:1])
 
@@ -94,7 +99,7 @@ def tile_block_attention_guide_pb_t_kernel(
             for n, spread_to in ((2, gain), (3, shift)):
                 spread = psum_turn.tile([P, C], F32, tag="turned")
                 nc.tensor.matmul(
-                    out=spread[:], lhsT=ones[:], rhs=vector_rows[:, n * C : (n + 1) * C], start=True, stop=True
+                    out=spread[:], lhsT=ones[:, 0:P], rhs=vector_rows[:, n * C : (n + 1) * C], start=True, stop=True
                 )
                 nc.scalar.copy(out=spread_to[:], in_=spread[:])
 
@@ -114,7 +119,10 @@ def tile_block_attention_guide_pb_t_kernel(
 
         def turn_weights(parts):
             for n in parts:
-                turned_w = psum_h.tile([P, 2, 2, P], F32, tag="h_acc")
+                if n < 2:
+                    turned_w = psum_h.tile([P, 2, 2, P], F32, tag="h_acc")
+                else:
+                    turned_w = psum_turn.tile([P, 2, 2, P], F32, tag="turned")
                 for m in range(2):
                     for u in range(2):
                         nc.tensor.transpose(
@@ -125,7 +133,7 @@ def tile_block_attention_guide_pb_t_kernel(
                 cols = slice(n * W_COLS * PACK, (n + 1) * W_COLS * PACK)
                 words_out = w_grouped[:, cols].bitcast(F32).rearrange("q (m p u) -> q m p u", m=2, u=2)
                 words_in = turned_w[:].rearrange("q m u p -> q m p u")
-                if n % 2 == 0:
+                if n == 0:
                     nc.vector.tensor_copy(out=words_out, in_=words_in)
                 else:
                     nc.scalar.copy(out=words_out, in_=words_in)
@@ -445,22 +453,50 @@ def tile_block_attention_guide_pb_t_kernel(
         def in_range(i):
             return 0 <= i < PAIRS
 
+        def first_step():
+            load_g1(3)
+            load_adj(2)
+            load_res(1)
+            for cc in range(CHUNKS):
+                add_bias(0, 0, cc)
+            quantise_a(adj_grouped[0], adj_packed[0], adj_padded[0])
+            quantise_weights(1)
+            for cc in range(CHUNKS):
+                conv(0, 1, cc)
+            scale_adj(1)
+            for cc in range(CHUNKS):
+                add_bias(0, 1, cc)
+                if cc == 1:
+                    quantise_a(spatial_grouped, spatial_packed, spatial_padded)
+                if cc == 2:
+                    quantise_g1(1)
+                    for chunk in range(CHUNKS):
+                        conv(1, 0, chunk)
+                    for half in range(2):
+                        turn_g1(2, half)
+                        group_g1(2, half)
+            quantise_h(0, 0)
+            quantise_h(0, 1)
+            aggregate(0, 0)
+            quantise_a(adj_grouped[1], adj_packed[1], adj_padded[1])
+
         def step(i):
-            before, next_one = (in_range(i - 1), in_range(i + 1))
+            next_one = in_range(i + 1)
             done = i - 2
             if in_range(i + 3):
                 load_g1(i + 3)
             if in_range(i + 2):
                 load_adj(i + 2)
-            if in_range(i + 1):
+            if next_one:
                 load_res(i + 1)
             if in_range(done):
                 for s, wt in ((0, 0), (0, 1), (1, 0), (1, 1)):
                     standardise(done, s, wt)
-                for vector, op in ((gain, ALU.mult), (shift, ALU.add)):
-                    gpsimd_apply(done, 0, slice(0, 2), vector, op)
-                    gpsimd_apply(done, 1, slice(0, 1), vector, op)
-                store_xn(done, 0)
+                gpsimd_apply(done, 0, slice(0, 1), gain, ALU.mult)
+                gpsimd_apply(done, 0, slice(1, 2), gain, ALU.mult)
+                gpsimd_apply(done, 1, slice(0, 1), gain, ALU.mult)
+                gpsimd_apply(done, 0, slice(0, 2), shift, ALU.add)
+                gpsimd_apply(done, 1, slice(0, 1), shift, ALU.add)
             for n in range(K * CHUNKS):
                 k, cc = divmod(n, CHUNKS)
                 add_bias(i, k, cc)
@@ -468,85 +504,97 @@ def tile_block_attention_guide_pb_t_kernel(
                     conv(i, 1, cc)
                 elif next_one:
                     conv(i + 1, 0, cc)
-                if n == 1 and before:
+                if n == 0 and i > 1 and next_one:
+                    scale_adj(i + 1)
+                if n == 1:
                     add_residual(i - 1, 0)
                     aggregate(i - 1, 1)
-                if n == 3 and i == 0:
-                    quantise_g1(1)
-                    turn_g1(2, 0)
-                    turn_g1(2, 1)
-                    group_g1(2, 0)
-                    group_g1(2, 1)
-                if n == 5 and i == 0:
-                    spread_norm()
-                if n == 6 and i == 0:
-                    quantise_a(spatial_grouped, spatial_packed, spatial_padded)
-                    quantise_a(adj_grouped[0], adj_packed[0], adj_padded[0])
-                if n == 1 and i > 0 and in_range(i + 2):
-                    group_g1(i + 2, 0)
-                    group_g1(i + 2, 1)
-                if n == 2 and next_one:
-                    scale_adj(i + 1)
-                if n == 2 and in_range(done):
-                    turn_forth(done, 1, 1)
-                if n == 3 and before:
-                    add_residual(i - 1, 1)
-                    negate_mean(i - 1)
+                    negate_mean(i - 1, 0)
                     square(i - 1, 0)
+                if n == 0 and in_range(done - 1):
+                    turn_back(done - 1, 1, 1)
+                    store_xn(done - 1, 1)
+                if n == 2 and in_range(i + 2):
+                    for half in range(2):
+                        turn_g1(i + 2, half)
+                        group_g1(i + 2, half)
+                if n == 3 and i == 1:
+                    quantise_g1(2)
+                    scale_adj(2)
+                if n == 4:
+                    add_residual(i - 1, 1)
+                    negate_mean(i - 1, 1)
                     square(i - 1, 1)
                     root(i - 1)
+                    if in_range(done):
+                        turn_forth(done, 1, 1)
+                if n == 5 and i == 1:
+                    spread_norm()
                 if n == 5 and in_range(done):
-                    turn_back(done, 1, 1)
-                    store_xn(done, 1)
-            if in_range(i + 2):
-                quantise_g1(i + 2)
+                    store_xn(done, 0)
             if next_one:
-                quantise_a(adj_grouped[i + 1], adj_packed[(i + 1) % 2], adj_padded[(i + 1) % 2])
-            quantise_h(i, 0)
-            if before:
+                quantise_h(i, 0)
+                quantise_h(i, 1)
+                aggregate(i, 0)
                 invert(i - 1)
-            quantise_h(i, 1)
-            aggregate(i, 0)
-            if before:
+                if in_range(i + 2):
+                    quantise_g1(i + 2)
                 offset_mean(i - 1)
-            if in_range(i + 3):
-                turn_g1(i + 3, 0)
-                turn_g1(i + 3, 1)
+                quantise_a(adj_grouped[i + 1], adj_packed[(i + 1) % 2], adj_padded[(i + 1) % 2])
+
+            else:
+                keep_warm(3)
+                quantise_h(i, 0)
+                quantise_h(i, 1)
+                aggregate(i, 0)
+                invert(i - 1)
+                offset_mean(i - 1)
+
+        def store_half(i, s, wt):
+            nc.sync.dma_start(
+                out=out_1[2 * i + s].rearrange("(m wt) c -> wt m c", wt=2)[wt], in_=xn_of(i, s)[:, wt, :]
+            )
 
         def finish():
             last = PAIRS - 1
             done = last - 1
-            for wt in range(2):
-                standardise(done, 0, wt)
-            for wt in range(2):
-                gpsimd_apply(done, 0, slice(wt, wt + 1), gain, ALU.mult)
-            for wt in range(2):
-                gpsimd_apply(done, 0, slice(wt, wt + 1), shift, ALU.add)
-            store_xn(done, 0)
+            for s, wt in ((0, 0), (0, 1), (1, 1)):
+                standardise(done, s, wt)
+            turn_back(done - 1, 1, 1)
+            store_xn(done - 1, 1)
             add_residual(last, 0)
             aggregate(last, 1)
             negate_mean(last, 0)
             square(last, 0)
             root(last, 0)
             add_residual(last, 1)
+            turn_forth(done, 0, 0)
             negate_mean(last, 1)
             square(last, 1)
             root(last, 1)
-            standardise(done, 1, 1)
-            turn_forth(done, 1, 1)
-            turn_back(done, 1, 1)
             vector_times_gain(done, 1, 0)
             invert(last, 0)
             vector_plus_shift(done, 1, 0)
-            store_xn(done, 1)
-            for s in range(2):
-                for wt in range(2):
-                    vector_times_gain(last, s, wt)
-                if s == 0:
-                    invert(last, 1)
-                for wt in range(2):
-                    vector_plus_shift(last, s, wt)
-                store_xn(last, s)
+            store_half(done, 1, 0)
+            turn_back(done, 0, 0)
+            store_half(done, 0, 0)
+            vector_times_gain(last, 0, 0)
+            vector_times_gain(last, 0, 1)
+            invert(last, 1)
+            for wt in range(2):
+                vector_plus_shift(last, 0, wt)
+                store_half(last, 0, wt)
+            turn_forth(done, 0, 1)
+            turn_back(done, 0, 1)
+            store_half(done, 0, 1)
+            vector_times_gain(last, 1, 0)
+            vector_times_gain(last, 1, 1)
+            for wt in range(2):
+                vector_plus_shift(last, 1, wt)
+                store_half(last, 1, wt)
+            turn_forth(done, 1, 1)
+            turn_back(done, 1, 1)
+            store_half(done, 1, 1)
 
         load_g1(0)
         load_weights((0, 1))
@@ -563,25 +611,24 @@ def tile_block_attention_guide_pb_t_kernel(
         load_adj(1)
 
         zero_other_rows()
-        turn_g1(0, 0)
-        turn_g1(0, 1)
-        group_g1(0, 0)
-        group_g1(0, 1)
+        keep_warm(5)
+        for half in range(2):
+            turn_g1(0, half)
+            group_g1(0, half)
         turn_weights((0, 1))
         quantise_g1(0)
-        spread_bias()
-        turn_weights((2, 3))
         quantise_weights(0)
-        quantise_weights(1)
+        spread_bias()
         spread_s2()
-        turn_g1(1, 0)
-        turn_g1(1, 1)
-        group_g1(1, 0)
-        group_g1(1, 1)
         for cc in range(CHUNKS):
             conv(0, 0, cc)
         scale_adj(0)
+        turn_weights((2, 3))
+        for half in range(2):
+            turn_g1(1, half)
+            group_g1(1, half)
         place_spatial()
-        for i in range(PAIRS):
+        first_step()
+        for i in range(1, PAIRS):
             step(i)
         finish()

@@ -57,8 +57,8 @@ def tile_block_attention_guide_pb_t_kernel(
             row = vector.rearrange("(o n) -> o n", o=1)
             nc.sync.dma_start(out=vector_rows[0:1, column : column + row.shape[1]], in_=row)
 
-        first_sqrt = consts.tile([P, 1], F32)
-        nc.scalar.activation(out=first_sqrt[:], in_=eps[:], func=ACT.Sqrt)
+        first_root = consts.tile([P, 1], F32)
+        nc.scalar.activation(out=first_root[:], in_=eps[:], func=ACT.Abs_reciprocal_sqrt)
 
         bias = consts.tile([P, K * C], BF16)
         gain = consts.tile([P, C], BF16)
@@ -204,7 +204,6 @@ def tile_block_attention_guide_pb_t_kernel(
         row_sum = {}
         neg_mean = {}
         squares = {}
-        std = {}
         rstd = {}
         offset = {}
         scaled_xn = {}
@@ -212,9 +211,13 @@ def tile_block_attention_guide_pb_t_kernel(
 
         def load_g1(i):
             g1_raw[i] = inputs.tile([P, PACK, C], BF16, tag="g1_raw", name="g1_raw%d" % i)
-            nc.sync.dma_start(
-                out=g1_raw[i][:], in_=g1[2 * i : 2 * i + 2].rearrange("b (r t) c -> (b r) t c", t=PACK)
-            )
+            rows = g1[2 * i : 2 * i + 2].rearrange("b (r t) c -> (b r) t c", t=PACK)
+            if i == 0:
+                for half in range(2):
+                    part = slice(2 * half, 2 * half + 2)
+                    nc.sync.dma_start(out=g1_raw[i][:, part], in_=rows[:, part])
+            else:
+                nc.sync.dma_start(out=g1_raw[i][:], in_=rows)
 
         def load_adj(i):
             adj_raw[i] = inputs.tile([P, PACK, J], BF16, tag="adj_raw", name="adj_raw%d" % i)
@@ -366,18 +369,16 @@ def tile_block_attention_guide_pb_t_kernel(
                 )
 
         def root(i, s=BOTH):
-            if i not in std:
-                deviation = stats.tile([P, 2, 2], F32, tag="std")
-                std[i] = deviation
-            nc.scalar.activation(
-                out=std[i][:, s, :], in_=squares[i][:, s, :], func=ACT.Sqrt, bias=eps[:], scale=1.0 / C
-            )
-
-        def invert(i, s=BOTH):
             if i not in rstd:
                 inverse = stats.tile([P, 2, 2], F32, tag="rstd")
                 rstd[i] = inverse
-            nc.vector.reciprocal(out=rstd[i][:, s, :], in_=std[i][:, s, :])
+            nc.scalar.activation(
+                out=rstd[i][:, s, :],
+                in_=squares[i][:, s, :],
+                func=ACT.Abs_reciprocal_sqrt,
+                bias=eps[:],
+                scale=1.0 / C,
+            )
 
         def offset_mean(i):
             product = stats.tile([P, 2, 2], F32, tag="offset")
@@ -463,21 +464,23 @@ def tile_block_attention_guide_pb_t_kernel(
             quantise_weights(1)
             for cc in range(CHUNKS):
                 conv(0, 1, cc)
+            for half in range(2):
+                turn_g1(1, half)
+                group_g1(1, half)
             scale_adj(1)
             for cc in range(CHUNKS):
                 add_bias(0, 1, cc)
                 if cc == 1:
                     quantise_a(spatial_grouped, spatial_packed, spatial_padded)
-                if cc == 2:
-                    quantise_g1(1)
-                    for chunk in range(CHUNKS):
-                        conv(1, 0, chunk)
-                    for half in range(2):
-                        turn_g1(2, half)
-                        group_g1(2, half)
             quantise_h(0, 0)
             quantise_h(0, 1)
             aggregate(0, 0)
+            quantise_g1(1)
+            for cc in range(CHUNKS):
+                conv(1, 0, cc)
+            for half in range(2):
+                turn_g1(2, half)
+                group_g1(2, half)
             quantise_a(adj_grouped[1], adj_packed[1], adj_padded[1])
 
         def step(i):
@@ -536,30 +539,24 @@ def tile_block_attention_guide_pb_t_kernel(
                 quantise_h(i, 0)
                 quantise_h(i, 1)
                 aggregate(i, 0)
-                invert(i - 1)
                 if in_range(i + 2):
                     quantise_g1(i + 2)
                 offset_mean(i - 1)
                 quantise_a(adj_grouped[i + 1], adj_packed[(i + 1) % 2], adj_padded[(i + 1) % 2])
 
             else:
-                keep_warm(3)
                 quantise_h(i, 0)
                 quantise_h(i, 1)
                 aggregate(i, 0)
-                invert(i - 1)
                 offset_mean(i - 1)
-
-        def store_half(i, s, wt):
-            nc.sync.dma_start(
-                out=out_1[2 * i + s].rearrange("(m wt) c -> wt m c", wt=2)[wt], in_=xn_of(i, s)[:, wt, :]
-            )
 
         def finish():
             last = PAIRS - 1
             done = last - 1
-            for s, wt in ((0, 0), (0, 1), (1, 1)):
+            for s, wt in ((0, 1), (0, 0), (1, 1)):
                 standardise(done, s, wt)
+            gpsimd_apply(done, 0, slice(1, 2), gain, ALU.mult)
+            gpsimd_apply(done, 0, slice(1, 2), shift, ALU.add)
             turn_back(done - 1, 1, 1)
             store_xn(done - 1, 1)
             add_residual(last, 0)
@@ -572,29 +569,23 @@ def tile_block_attention_guide_pb_t_kernel(
             negate_mean(last, 1)
             square(last, 1)
             root(last, 1)
-            vector_times_gain(done, 1, 0)
-            invert(last, 0)
-            vector_plus_shift(done, 1, 0)
-            store_half(done, 1, 0)
-            turn_back(done, 0, 0)
-            store_half(done, 0, 0)
             vector_times_gain(last, 0, 0)
             vector_times_gain(last, 0, 1)
-            invert(last, 1)
+            vector_times_gain(done, 1, 0)
+            vector_plus_shift(done, 1, 0)
             for wt in range(2):
                 vector_plus_shift(last, 0, wt)
-                store_half(last, 0, wt)
-            turn_forth(done, 0, 1)
-            turn_back(done, 0, 1)
-            store_half(done, 0, 1)
+            store_xn(last, 0)
+            turn_back(done, 0, 0)
+            store_xn(done, 0)
+            turn_forth(done, 1, 1)
+            turn_back(done, 1, 1)
+            store_xn(done, 1)
             vector_times_gain(last, 1, 0)
             vector_times_gain(last, 1, 1)
             for wt in range(2):
                 vector_plus_shift(last, 1, wt)
-                store_half(last, 1, wt)
-            turn_forth(done, 1, 1)
-            turn_back(done, 1, 1)
-            store_half(done, 1, 1)
+            store_xn(last, 1)
 
         load_g1(0)
         load_weights((0, 1))
@@ -611,7 +602,7 @@ def tile_block_attention_guide_pb_t_kernel(
         load_adj(1)
 
         zero_other_rows()
-        keep_warm(5)
+        keep_warm(4)
         for half in range(2):
             turn_g1(0, half)
             group_g1(0, half)
@@ -624,9 +615,6 @@ def tile_block_attention_guide_pb_t_kernel(
             conv(0, 0, cc)
         scale_adj(0)
         turn_weights((2, 3))
-        for half in range(2):
-            turn_g1(1, half)
-            group_g1(1, half)
         place_spatial()
         first_step()
         for i in range(1, PAIRS):

@@ -524,7 +524,7 @@ def tile_block_attention_guide_pb_t_kernel(
                 if n == 3 and i == 1:
                     quantise_g1(2)
                     scale_adj(2)
-                if n == 4:
+                if n == (4 if next_one else 2):
                     add_residual(i - 1, 1)
                     negate_mean(i - 1, 1)
                     square(i - 1, 1)
@@ -533,6 +533,16 @@ def tile_block_attention_guide_pb_t_kernel(
                         turn_forth(done, 1, 1)
                 if n == 5 and i == 1:
                     spread_norm()
+                if n == 6 and not next_one:
+                    turn_back(done, 1, 1)
+                    store_xn(done, 1)
+                    offset_mean(i - 1)
+                    for s, wt in ((0, 1), (0, 0), (1, 1)):
+                        standardise(i - 1, s, wt)
+                    gpsimd_apply(i - 1, 0, slice(1, 2), gain, ALU.mult)
+                    gpsimd_apply(i - 1, 0, slice(1, 2), shift, ALU.add)
+                if n == 99 and not next_one:
+                    turn_forth(i - 1, 0, 0)
                 if n == 5 and in_range(done):
                     store_xn(done, 0)
             if next_one:
@@ -548,44 +558,42 @@ def tile_block_attention_guide_pb_t_kernel(
                 quantise_h(i, 0)
                 quantise_h(i, 1)
                 aggregate(i, 0)
-                offset_mean(i - 1)
+
+        def store_half(i, s, wt):
+            nc.sync.dma_start(
+                out=out_1[2 * i + s].rearrange("(m wt) c -> wt m c", wt=2)[wt], in_=xn_of(i, s)[:, wt, :]
+            )
 
         def finish():
             last = PAIRS - 1
             done = last - 1
-            for s, wt in ((0, 1), (0, 0), (1, 1)):
-                standardise(done, s, wt)
-            gpsimd_apply(done, 0, slice(1, 2), gain, ALU.mult)
-            gpsimd_apply(done, 0, slice(1, 2), shift, ALU.add)
-            turn_back(done - 1, 1, 1)
-            store_xn(done - 1, 1)
             add_residual(last, 0)
             aggregate(last, 1)
             negate_mean(last, 0)
             square(last, 0)
             root(last, 0)
-            add_residual(last, 1)
             turn_forth(done, 0, 0)
+            add_residual(last, 1)
             negate_mean(last, 1)
             square(last, 1)
             root(last, 1)
             vector_times_gain(last, 0, 0)
             vector_times_gain(last, 0, 1)
-            vector_times_gain(done, 1, 0)
-            vector_plus_shift(done, 1, 0)
             for wt in range(2):
                 vector_plus_shift(last, 0, wt)
             store_xn(last, 0)
+            turn_forth(done, 1, 1)
             turn_back(done, 0, 0)
             store_xn(done, 0)
-            turn_forth(done, 1, 1)
+            vector_times_gain(done, 1, 0)
+            vector_times_gain(last, 1, 0)
+            vector_plus_shift(done, 1, 0)
             turn_back(done, 1, 1)
             store_xn(done, 1)
-            vector_times_gain(last, 1, 0)
             vector_times_gain(last, 1, 1)
             for wt in range(2):
                 vector_plus_shift(last, 1, wt)
-            store_xn(last, 1)
+                store_half(last, 1, wt)
 
         load_g1(0)
         load_weights((0, 1))

@@ -36,7 +36,7 @@ def tile_block_attention_guide_pb_t_kernel(
         inputs = ctx.enter_context(tc.tile_pool(name="inputs", bufs=4))
         stage = ctx.enter_context(tc.tile_pool(name="stage", bufs=2))
         packed = ctx.enter_context(tc.tile_pool(name="packed", bufs=3))
-        results = ctx.enter_context(tc.tile_pool(name="results", bufs=8))
+        results = ctx.enter_context(tc.tile_pool(name="results", bufs=4))
         stats = ctx.enter_context(tc.tile_pool(name="stats", bufs=6))
         psum_turn = ctx.enter_context(tc.psum_pool(name="psum_turn", bufs=2))
         psum_h = ctx.enter_context(tc.psum_pool(name="psum_h", bufs=4))
@@ -227,10 +227,10 @@ def tile_block_attention_guide_pb_t_kernel(
 
         def load_res(i):
             res_raw[i] = inputs.tile([P, 2, 2, C], BF16, tag="res_raw", name="res_raw%d" % i)
-            for s in range(2):
-                nc.sync.dma_start(
-                    out=res_raw[i][:, s], in_=res1[2 * i + s].rearrange("(m wt) c -> m wt c", wt=2)
-                )
+            nc.sync.dma_start(
+                out=res_raw[i][:].rearrange("p s wt c -> p s (wt c)"),
+                in_=res1[2 * i : 2 * i + 2].rearrange("s (m wt) c -> m s (wt c)", wt=2),
+            )
 
         def turn_g1(i, half):
             turned = psum_turn.tile([P, 2, 2, P], F32, tag="turned")
@@ -262,12 +262,14 @@ def tile_block_attention_guide_pb_t_kernel(
 
         def scale_adj(i):
             grouped = stage.tile([P, J, PACK], BF16, tag="adj_grouped", align_bytes=64)
-            nc.scalar.activation(
-                out=grouped[:].rearrange("p (wt m) t -> p wt m t", wt=2),
-                in_=adj_raw[i][:].rearrange("p t (m wt) -> p wt m t", wt=2),
-                func=ACT.Copy,
-                scale=s2_f32[:],
-            )
+            source = adj_raw[i][:].rearrange("p t (m wt) -> p wt m t", wt=2)
+            target = grouped[:].rearrange("p (wt m) t -> p wt m t", wt=2)
+            if i < 2:
+                nc.scalar.activation(out=target, in_=source, func=ACT.Copy, scale=s2_f32[:])
+            else:
+                nc.gpsimd.tensor_scalar(
+                    out=target, in0=source, scalar1=s2_f32[:], scalar2=0.0, op0=ALU.mult, op1=ALU.add
+                )
             adj_grouped[i] = grouped
 
         def conv(i, k, cc):
@@ -326,13 +328,14 @@ def tile_block_attention_guide_pb_t_kernel(
                 g2_acc[(i, s, wt)] = acc
 
         def add_residual(i, s):
-            x2_tile = results.tile([P, 2, C], F32, tag="x2")
             if s == 0:
+                x2_tile = results.tile([P, 2, 2, C], F32, tag="x2")
+                x2[i] = x2_tile
                 sums = stats.tile([P, 2, 2], F32, tag="row_sum")
                 row_sum[i] = sums
             for wt in range(2):
                 nc.vector.scalar_tensor_tensor(
-                    out=x2_tile[:, wt, :],
+                    out=x2[i][:, s, wt, :],
                     in0=g2_acc[(i, s, wt)][:],
                     scalar=1.0,
                     in1=res_raw[i][:, s, wt, :],
@@ -340,10 +343,19 @@ def tile_block_attention_guide_pb_t_kernel(
                     op1=ALU.add,
                     accum_out=row_sum[i][:, s, wt : wt + 1],
                 )
+            if i == PAIRS - 1:
+                store_sample(out_0, i, s, x2[i])
+            elif s == 1:
+                store_pair(out_0, i, x2[i])
+
+        def store_pair(out, i, tile):
             nc.sync.dma_start(
-                out=out_0[2 * i + s].rearrange("(m wt) c -> m wt c", wt=2), in_=x2_tile[:]
+                out=out[2 * i : 2 * i + 2].rearrange("s (m wt) c -> m s (wt c)", wt=2),
+                in_=tile[:].rearrange("p s wt c -> p s (wt c)"),
             )
-            x2[(i, s)] = x2_tile
+
+        def store_sample(out, i, s, tile):
+            nc.sync.dma_start(out=out[2 * i + s].rearrange("(m wt) c -> m wt c", wt=2), in_=tile[:, s])
 
         BOTH = slice(0, 2)
 
@@ -361,7 +373,7 @@ def tile_block_attention_guide_pb_t_kernel(
                 unread = stats.tile([P, C], BF16, tag="unread")
                 nc.scalar.activation(
                     out=unread[:],
-                    in_=x2[(i, s)][:, wt, :],
+                    in_=x2[i][:, s, wt, :],
                     func=ACT.Square,
                     bias=neg_mean[i][:, s, wt : wt + 1],
                     scale=1.0,
@@ -385,16 +397,16 @@ def tile_block_attention_guide_pb_t_kernel(
             nc.vector.tensor_tensor(out=product[:], in0=neg_mean[i][:], in1=rstd[i][:], op=ALU.mult)
             offset[i] = product
 
-        def xn_of(i, s):
-            if (i, s) not in xn_tile:
-                xn = results.tile([P, 2, C], F32, tag="xn")
-                xn_tile[(i, s)] = xn
-            return xn_tile[(i, s)]
+        def xn_of(i):
+            if i not in xn_tile:
+                xn = results.tile([P, 2, 2, C], F32, tag="xn")
+                xn_tile[i] = xn
+            return xn_tile[i]
 
         def vector_times_gain(i, s, wt):
             nc.vector.scalar_tensor_tensor(
-                out=xn_of(i, s)[:, wt, :],
-                in0=x2[(i, s)][:, wt, :],
+                out=xn_of(i)[:, s, wt, :],
+                in0=x2[i][:, s, wt, :],
                 scalar=neg_mean[i][:, s, wt : wt + 1],
                 in1=gain[:],
                 op0=ALU.add,
@@ -403,8 +415,8 @@ def tile_block_attention_guide_pb_t_kernel(
 
         def vector_plus_shift(i, s, wt):
             nc.vector.scalar_tensor_tensor(
-                out=xn_of(i, s)[:, wt, :],
-                in0=xn_of(i, s)[:, wt, :],
+                out=xn_of(i)[:, s, wt, :],
+                in0=xn_of(i)[:, s, wt, :],
                 scalar=rstd[i][:, s, wt : wt + 1],
                 in1=shift[:],
                 op0=ALU.mult,
@@ -413,8 +425,8 @@ def tile_block_attention_guide_pb_t_kernel(
 
         def standardise(i, s, wt):
             nc.scalar.activation(
-                out=xn_of(i, s)[:, wt, :],
-                in_=x2[(i, s)][:, wt, :],
+                out=xn_of(i)[:, s, wt, :],
+                in_=x2[i][:, s, wt, :],
                 func=ACT.Identity,
                 bias=offset[i][:, s, wt : wt + 1],
                 scale=rstd[i][:, s, wt : wt + 1],
@@ -423,8 +435,8 @@ def tile_block_attention_guide_pb_t_kernel(
         def turn_forth(i, s, wt):
             turned = psum_turn.tile([P, CHUNKS, P], F32, tag="turned")
             for cc in range(CHUNKS):
-                nc.tensor.transpose(turned[:, cc, :], xn_of(i, s)[:, wt, cc * P : (cc + 1) * P], identity[:])
-            scaled = stage.tile([P, CHUNKS, P], F32, tag="scaled")
+                nc.tensor.transpose(turned[:, cc, :], xn_of(i)[:, s, wt, cc * P : (cc + 1) * P], identity[:])
+            scaled = stage.tile([P, CHUNKS, P], F32, tag="scaled%d%d" % (s, wt))
             for cc in range(CHUNKS):
                 nc.scalar.activation(
                     out=scaled[:, cc, :],
@@ -439,17 +451,14 @@ def tile_block_attention_guide_pb_t_kernel(
             turned = psum_turn.tile([P, CHUNKS, P], F32, tag="turned")
             for cc in range(CHUNKS):
                 nc.tensor.transpose(turned[:, cc, :], scaled_xn[(i, s, wt)][:, cc, :], identity[:])
-            nc.scalar.copy(out=xn_of(i, s)[:, wt, :], in_=turned[:].rearrange("p c n -> p (c n)"))
+            nc.scalar.copy(out=xn_of(i)[:, s, wt, :], in_=turned[:].rearrange("p c n -> p (c n)"))
 
         def gpsimd_apply(i, s, wts, vector, op):
-            part = xn_of(i, s)[:, wts, :]
+            part = xn_of(i)[:, s, wts, :]
             many = wts.stop - wts.start
             nc.gpsimd.tensor_tensor(
                 out=part, in0=part, in1=vector[:].unsqueeze(1).to_broadcast([P, many, C]), op=op
             )
-
-        def store_xn(i, s):
-            nc.sync.dma_start(out=out_1[2 * i + s].rearrange("(m wt) c -> m wt c", wt=2), in_=xn_of(i, s)[:])
 
         def in_range(i):
             return 0 <= i < PAIRS
@@ -497,9 +506,7 @@ def tile_block_attention_guide_pb_t_kernel(
                     standardise(done, s, wt)
                 gpsimd_apply(done, 0, slice(0, 1), gain, ALU.mult)
                 gpsimd_apply(done, 0, slice(1, 2), gain, ALU.mult)
-                gpsimd_apply(done, 1, slice(0, 1), gain, ALU.mult)
                 gpsimd_apply(done, 0, slice(0, 2), shift, ALU.add)
-                gpsimd_apply(done, 1, slice(0, 1), shift, ALU.add)
             for n in range(K * CHUNKS):
                 k, cc = divmod(n, CHUNKS)
                 add_bias(i, k, cc)
@@ -515,8 +522,9 @@ def tile_block_attention_guide_pb_t_kernel(
                     negate_mean(i - 1, 0)
                     square(i - 1, 0)
                 if n == 0 and in_range(done - 1):
+                    turn_back(done - 1, 1, 0)
                     turn_back(done - 1, 1, 1)
-                    store_xn(done - 1, 1)
+                    store_pair(out_1, done - 1, xn_of(done - 1))
                 if n == 2 and in_range(i + 2):
                     for half in range(2):
                         turn_g1(i + 2, half)
@@ -530,12 +538,14 @@ def tile_block_attention_guide_pb_t_kernel(
                     square(i - 1, 1)
                     root(i - 1)
                     if in_range(done):
+                        turn_forth(done, 1, 0)
                         turn_forth(done, 1, 1)
                 if n == 5 and i == 1:
                     spread_norm()
                 if n == 6 and not next_one:
+                    turn_back(done, 1, 0)
                     turn_back(done, 1, 1)
-                    store_xn(done, 1)
+                    store_pair(out_1, done, xn_of(done))
                     offset_mean(i - 1)
                     for s, wt in ((0, 1), (0, 0), (1, 1)):
                         standardise(i - 1, s, wt)
@@ -543,8 +553,6 @@ def tile_block_attention_guide_pb_t_kernel(
                     gpsimd_apply(i - 1, 0, slice(1, 2), shift, ALU.add)
                 if n == 99 and not next_one:
                     turn_forth(i - 1, 0, 0)
-                if n == 5 and in_range(done):
-                    store_xn(done, 0)
             if next_one:
                 quantise_h(i, 0)
                 quantise_h(i, 1)
@@ -561,7 +569,7 @@ def tile_block_attention_guide_pb_t_kernel(
 
         def store_half(i, s, wt):
             nc.sync.dma_start(
-                out=out_1[2 * i + s].rearrange("(m wt) c -> wt m c", wt=2)[wt], in_=xn_of(i, s)[:, wt, :]
+                out=out_1[2 * i + s].rearrange("(m wt) c -> wt m c", wt=2)[wt], in_=xn_of(i)[:, s, wt, :]
             )
 
         def finish():
@@ -581,15 +589,15 @@ def tile_block_attention_guide_pb_t_kernel(
             vector_times_gain(last, 0, 1)
             for wt in range(2):
                 vector_plus_shift(last, 0, wt)
-            store_xn(last, 0)
+            store_sample(out_1, last, 0, xn_of(last))
             turn_forth(done, 1, 1)
             turn_back(done, 0, 0)
-            store_xn(done, 0)
+            store_sample(out_1, done, 0, xn_of(done))
             vector_times_gain(done, 1, 0)
             vector_times_gain(last, 1, 0)
             vector_plus_shift(done, 1, 0)
             turn_back(done, 1, 1)
-            store_xn(done, 1)
+            store_sample(out_1, done, 1, xn_of(done))
             vector_times_gain(last, 1, 1)
             for wt in range(2):
                 vector_plus_shift(last, 1, wt)

@@ -19,10 +19,15 @@ K = 2
 EPS = 1e-5
 P = 128
 PAIRS = B // 2
+LAST = PAIRS - 1
 HALF = P // 2
 PACK = 4
 CHUNKS = C // P
-S2_COLS = 64
+A_WORDS = J + J // PACK
+W_PARTS = 4
+THIN = 64
+WARM_MATMULS = 4
+SCALAR_ADJ_PAIRS = 2
 
 FLOPS = 2 * B * J * C * (K * C) + 2 * B * (K * J) * J * C
 
@@ -48,7 +53,7 @@ def tile_block_attention_guide_pb_t_kernel(
         eps = consts.tile([P, 1], F32)
         nc.vector.memset(eps[:], EPS)
 
-        vector_rows = consts.tile([P, 4 * C + S2_COLS], BF16)
+        vector_rows = consts.tile([P, 4 * C + THIN], BF16)
         nc.vector.memset(vector_rows[:].bitcast(I32), 0)
         ones = consts.tile([P, C], BF16)
         nc.vector.memset(ones[:], 1.0)
@@ -67,44 +72,40 @@ def tile_block_attention_guide_pb_t_kernel(
         columns = consts.tile([P, 2 * CHUNKS], F32)
 
         def keep_warm(times):
-            idle = psum_g2.tile([P, C], F32, tag="g2_acc")
+            unread = psum_g2.tile([P, C], F32, tag="g2_acc")
             for n in range(times):
-                nc.tensor.matmul(out=idle[:], lhsT=ones[:, 0:P], rhs=ones[:], start=True, stop=True)
+                nc.tensor.matmul(out=unread[:], lhsT=ones[:, 0:P], rhs=ones[:], start=True, stop=True)
 
         def spread_bias():
             for k in range(K):
                 spread = psum_g2.tile([P, C], F32, tag="g2_acc")
+                cols = slice(k * C, (k + 1) * C)
                 nc.tensor.matmul(
-                    out=spread[:], lhsT=ones[:, 0:P], rhs=vector_rows[:, k * C : (k + 1) * C], start=True, stop=True
+                    out=spread[:], lhsT=ones[:, 0:P], rhs=vector_rows[:, cols], start=True, stop=True
                 )
-                nc.scalar.copy(out=bias[:, k * C : (k + 1) * C], in_=spread[:])
+                nc.scalar.copy(out=bias[:, cols], in_=spread[:])
+
         def spread_s2():
-            spread = psum_g2.tile([P, S2_COLS], F32, tag="g2_acc")
+            spread = psum_g2.tile([P, THIN], F32, tag="g2_acc")
             nc.tensor.matmul(
                 out=spread[:], lhsT=ones[:, 0:P], rhs=vector_rows[:, 4 * C :], start=True, stop=True
             )
             nc.scalar.copy(out=s2_f32[:], in_=spread[:, 0:1])
 
         def spread_norm():
-            spread = psum_turn.tile([P, 2 * CHUNKS, S2_COLS], F32, tag="turned")
+            spread = psum_turn.tile([P, 2 * CHUNKS, THIN], F32, tag="turned")
             for n in range(2 * CHUNKS):
-                nc.tensor.matmul(
-                    out=spread[:, n, :],
-                    lhsT=vector_rows[:, 2 * C + n * P : 2 * C + (n + 1) * P],
-                    rhs=ones[:, 0:S2_COLS],
-                    start=True,
-                    stop=True,
-                )
+                row = vector_rows[:, 2 * C + n * P : 2 * C + (n + 1) * P]
+                nc.tensor.matmul(out=spread[:, n, :], lhsT=row, rhs=ones[:, 0:THIN], start=True, stop=True)
             nc.scalar.copy(out=columns[:], in_=spread[:, :, 0])
             for n, spread_to in ((2, gain), (3, shift)):
                 spread = psum_turn.tile([P, C], F32, tag="turned")
+                cols = slice(n * C, (n + 1) * C)
                 nc.tensor.matmul(
-                    out=spread[:], lhsT=ones[:, 0:P], rhs=vector_rows[:, n * C : (n + 1) * C], start=True, stop=True
+                    out=spread[:], lhsT=ones[:, 0:P], rhs=vector_rows[:, cols], start=True, stop=True
                 )
                 nc.scalar.copy(out=spread_to[:], in_=spread[:])
 
-        W_PARTS = 4
-        W_COLS = K * C // W_PARTS
         w_raw = consts.tile([P, W_PARTS, 2, C], BF16)
         w_grouped = consts.tile([P, K * C * PACK], BF16, align_bytes=64)
         w_codes = consts.tile([P, K * C], U32, align_bytes=64)
@@ -119,7 +120,7 @@ def tile_block_attention_guide_pb_t_kernel(
 
         def turn_weights(parts):
             for n in parts:
-                if n < 2:
+                if n < W_PARTS // K:
                     turned_w = psum_h.tile([P, 2, 2, P], F32, tag="h_acc")
                 else:
                     turned_w = psum_turn.tile([P, 2, 2, P], F32, tag="turned")
@@ -130,7 +131,8 @@ def tile_block_attention_guide_pb_t_kernel(
                             w_raw[:, n, m, :].bitcast(F32)[:, u : 2 * P : 2],
                             identity[:],
                         )
-                cols = slice(n * W_COLS * PACK, (n + 1) * W_COLS * PACK)
+                width = K * C * PACK // W_PARTS
+                cols = slice(n * width, (n + 1) * width)
                 words_out = w_grouped[:, cols].bitcast(F32).rearrange("q (m p u) -> q m p u", m=2, u=2)
                 words_in = turned_w[:].rearrange("q m u p -> q m p u")
                 if n == 0:
@@ -139,16 +141,18 @@ def tile_block_attention_guide_pb_t_kernel(
                     nc.scalar.copy(out=words_out, in_=words_in)
 
         def quantise_weights(k):
-            if True:
-                nc.vector.quantize_mx(
-                    out=w_codes[:, k * C : (k + 1) * C].bitcast(FP8X4),
-                    scales=w_scales[:, k * C : (k + 1) * C],
-                    in_=w_grouped[:, k * C * PACK : (k + 1) * C * PACK],
-                )
+            nc.vector.quantize_mx(
+                out=w_codes[:, k * C : (k + 1) * C].bitcast(FP8X4),
+                scales=w_scales[:, k * C : (k + 1) * C],
+                in_=w_grouped[:, k * C * PACK : (k + 1) * C * PACK],
+            )
 
-        A_WORDS = J + J // PACK
-        adj_packed = [consts.tile([P, A_WORDS], U32, name="adj_packed%d" % n, align_bytes=64) for n in range(2)]
-        adj_padded = [consts.tile([P, 2, A_WORDS], U32, name="adj_padded%d" % n, align_bytes=64) for n in range(2)]
+        adj_packed = [
+            consts.tile([P, A_WORDS], U32, name="adj_packed%d" % n, align_bytes=64) for n in range(2)
+        ]
+        adj_padded = [
+            consts.tile([P, 2, A_WORDS], U32, name="adj_padded%d" % n, align_bytes=64) for n in range(2)
+        ]
         spatial_packed = consts.tile([P, A_WORDS], U32, align_bytes=64)
         spatial_padded = consts.tile([P, 2, A_WORDS], U32, align_bytes=64)
         spatial_raw = consts.tile([P, PACK, J], BF16)
@@ -264,7 +268,7 @@ def tile_block_attention_guide_pb_t_kernel(
             grouped = stage.tile([P, J, PACK], BF16, tag="adj_grouped", align_bytes=64)
             source = adj_raw[i][:].rearrange("p t (m wt) -> p wt m t", wt=2)
             target = grouped[:].rearrange("p (wt m) t -> p wt m t", wt=2)
-            if i < 2:
+            if i < SCALAR_ADJ_PAIRS:
                 nc.scalar.activation(out=target, in_=source, func=ACT.Copy, scale=s2_f32[:])
             else:
                 nc.gpsimd.tensor_scalar(
@@ -343,7 +347,7 @@ def tile_block_attention_guide_pb_t_kernel(
                     op1=ALU.add,
                     accum_out=row_sum[i][:, s, wt : wt + 1],
                 )
-            if i == PAIRS - 1:
+            if i == LAST:
                 store_sample(out_0, i, s, x2[i])
             elif s == 1:
                 store_pair(out_0, i, x2[i])
@@ -357,13 +361,20 @@ def tile_block_attention_guide_pb_t_kernel(
         def store_sample(out, i, s, tile):
             nc.sync.dma_start(out=out[2 * i + s].rearrange("(m wt) c -> m wt c", wt=2), in_=tile[:, s])
 
+        def store_half(out, i, s, wt, tile):
+            nc.sync.dma_start(
+                out=out[2 * i + s].rearrange("(m wt) c -> wt m c", wt=2)[wt], in_=tile[:, s, wt, :]
+            )
+
         BOTH = slice(0, 2)
 
-        def negate_mean(i, s=BOTH):
+        def negate_mean(i, s):
             if i not in neg_mean:
                 minus_mean = stats.tile([P, 2, 2], F32, tag="neg_mean")
                 neg_mean[i] = minus_mean
-            nc.scalar.activation(out=neg_mean[i][:, s, :], in_=row_sum[i][:, s, :], func=ACT.Copy, scale=-1.0 / C)
+            nc.scalar.activation(
+                out=neg_mean[i][:, s, :], in_=row_sum[i][:, s, :], func=ACT.Copy, scale=-1.0 / C
+            )
 
         def square(i, s):
             if i not in squares:
@@ -380,7 +391,7 @@ def tile_block_attention_guide_pb_t_kernel(
                     accum_out=squares[i][:, s, wt : wt + 1],
                 )
 
-        def root(i, s=BOTH):
+        def root(i, s):
             if i not in rstd:
                 inverse = stats.tile([P, 2, 2], F32, tag="rstd")
                 rstd[i] = inverse
@@ -445,7 +456,29 @@ def tile_block_attention_guide_pb_t_kernel(
                     bias=columns[:, CHUNKS + cc : CHUNKS + cc + 1],
                     scale=columns[:, cc : cc + 1],
                 )
-            scaled_xn[(i, s, wt)] = scaled
+            scaled_xn[(i, s, wt)] = scaled[:]
+
+        def turn_forth_both(i):
+            scaled = stage.tile([P, CHUNKS, 2, P], F32, tag="scaled_both")
+            for half in range(2):
+                turned = psum_turn.tile([P, 2, 2, P], F32, tag="turned")
+                for n in range(2):
+                    cc = 2 * half + n
+                    for wt in range(2):
+                        nc.tensor.transpose(
+                            turned[:, n, wt, :], xn_of(i)[:, 1, wt, cc * P : (cc + 1) * P], identity[:]
+                        )
+                for n in range(2):
+                    cc = 2 * half + n
+                    nc.scalar.activation(
+                        out=scaled[:, cc],
+                        in_=turned[:, n],
+                        func=ACT.Identity,
+                        bias=columns[:, CHUNKS + cc : CHUNKS + cc + 1],
+                        scale=columns[:, cc : cc + 1],
+                    )
+            for wt in range(2):
+                scaled_xn[(i, 1, wt)] = scaled[:, :, wt, :]
 
         def turn_back(i, s, wt):
             turned = psum_turn.tile([P, CHUNKS, P], F32, tag="turned")
@@ -459,6 +492,12 @@ def tile_block_attention_guide_pb_t_kernel(
             nc.gpsimd.tensor_tensor(
                 out=part, in0=part, in1=vector[:].unsqueeze(1).to_broadcast([P, many, C]), op=op
             )
+
+        def apply_on_vector(i, s, wts):
+            for wt in wts:
+                vector_times_gain(i, s, wt)
+            for wt in wts:
+                vector_plus_shift(i, s, wt)
 
         def in_range(i):
             return 0 <= i < PAIRS
@@ -493,17 +532,18 @@ def tile_block_attention_guide_pb_t_kernel(
             quantise_a(adj_grouped[1], adj_packed[1], adj_padded[1])
 
         def step(i):
-            next_one = in_range(i + 1)
+            last = i == LAST
             done = i - 2
             if in_range(i + 3):
                 load_g1(i + 3)
             if in_range(i + 2):
                 load_adj(i + 2)
-            if next_one:
+            if not last:
                 load_res(i + 1)
             if in_range(done):
-                for s, wt in ((0, 0), (0, 1), (1, 0), (1, 1)):
-                    standardise(done, s, wt)
+                for s in range(2):
+                    for wt in range(2):
+                        standardise(done, s, wt)
                 gpsimd_apply(done, 0, slice(0, 1), gain, ALU.mult)
                 gpsimd_apply(done, 0, slice(1, 2), gain, ALU.mult)
                 gpsimd_apply(done, 0, slice(0, 2), shift, ALU.add)
@@ -512,19 +552,19 @@ def tile_block_attention_guide_pb_t_kernel(
                 add_bias(i, k, cc)
                 if k == 0:
                     conv(i, 1, cc)
-                elif next_one:
+                elif not last:
                     conv(i + 1, 0, cc)
-                if n == 0 and i > 1 and next_one:
+                if n == 0 and i > 1 and not last:
                     scale_adj(i + 1)
+                if n == 0 and in_range(done - 1):
+                    for wt in range(2):
+                        turn_back(done - 1, 1, wt)
+                    store_pair(out_1, done - 1, xn_of(done - 1))
                 if n == 1:
                     add_residual(i - 1, 0)
                     aggregate(i - 1, 1)
                     negate_mean(i - 1, 0)
                     square(i - 1, 0)
-                if n == 0 and in_range(done - 1):
-                    turn_back(done - 1, 1, 0)
-                    turn_back(done - 1, 1, 1)
-                    store_pair(out_1, done - 1, xn_of(done - 1))
                 if n == 2 and in_range(i + 2):
                     for half in range(2):
                         turn_g1(i + 2, half)
@@ -532,76 +572,59 @@ def tile_block_attention_guide_pb_t_kernel(
                 if n == 3 and i == 1:
                     quantise_g1(2)
                     scale_adj(2)
-                if n == (4 if next_one else 2):
+                if n == (2 if last else 4):
                     add_residual(i - 1, 1)
                     negate_mean(i - 1, 1)
                     square(i - 1, 1)
-                    root(i - 1)
+                    root(i - 1, BOTH)
                     if in_range(done):
-                        turn_forth(done, 1, 0)
-                        turn_forth(done, 1, 1)
+                        turn_forth_both(done)
                 if n == 5 and i == 1:
                     spread_norm()
-                if n == 6 and not next_one:
-                    turn_back(done, 1, 0)
-                    turn_back(done, 1, 1)
+                if n == 6 and last:
+                    for wt in range(2):
+                        turn_back(done, 1, wt)
                     store_pair(out_1, done, xn_of(done))
                     offset_mean(i - 1)
                     for s, wt in ((0, 1), (0, 0), (1, 1)):
                         standardise(i - 1, s, wt)
                     gpsimd_apply(i - 1, 0, slice(1, 2), gain, ALU.mult)
                     gpsimd_apply(i - 1, 0, slice(1, 2), shift, ALU.add)
-                if n == 99 and not next_one:
-                    turn_forth(i - 1, 0, 0)
-            if next_one:
-                quantise_h(i, 0)
-                quantise_h(i, 1)
-                aggregate(i, 0)
-                if in_range(i + 2):
-                    quantise_g1(i + 2)
+            quantise_h(i, 0)
+            quantise_h(i, 1)
+            aggregate(i, 0)
+            if in_range(i + 2):
+                quantise_g1(i + 2)
+            if not last:
                 offset_mean(i - 1)
                 quantise_a(adj_grouped[i + 1], adj_packed[(i + 1) % 2], adj_padded[(i + 1) % 2])
 
-            else:
-                quantise_h(i, 0)
-                quantise_h(i, 1)
-                aggregate(i, 0)
-
-        def store_half(i, s, wt):
-            nc.sync.dma_start(
-                out=out_1[2 * i + s].rearrange("(m wt) c -> wt m c", wt=2)[wt], in_=xn_of(i)[:, s, wt, :]
-            )
-
         def finish():
-            last = PAIRS - 1
-            done = last - 1
-            add_residual(last, 0)
-            aggregate(last, 1)
-            negate_mean(last, 0)
-            square(last, 0)
-            root(last, 0)
+            done = LAST - 1
+            add_residual(LAST, 0)
+            aggregate(LAST, 1)
+            negate_mean(LAST, 0)
+            square(LAST, 0)
+            root(LAST, 0)
             turn_forth(done, 0, 0)
-            add_residual(last, 1)
-            negate_mean(last, 1)
-            square(last, 1)
-            root(last, 1)
-            vector_times_gain(last, 0, 0)
-            vector_times_gain(last, 0, 1)
-            for wt in range(2):
-                vector_plus_shift(last, 0, wt)
-            store_sample(out_1, last, 0, xn_of(last))
+            add_residual(LAST, 1)
+            negate_mean(LAST, 1)
+            square(LAST, 1)
+            root(LAST, 1)
+            apply_on_vector(LAST, 0, (0, 1))
+            store_sample(out_1, LAST, 0, xn_of(LAST))
             turn_forth(done, 1, 1)
             turn_back(done, 0, 0)
             store_sample(out_1, done, 0, xn_of(done))
             vector_times_gain(done, 1, 0)
-            vector_times_gain(last, 1, 0)
+            vector_times_gain(LAST, 1, 0)
             vector_plus_shift(done, 1, 0)
             turn_back(done, 1, 1)
             store_sample(out_1, done, 1, xn_of(done))
-            vector_times_gain(last, 1, 1)
+            vector_times_gain(LAST, 1, 1)
             for wt in range(2):
-                vector_plus_shift(last, 1, wt)
-                store_half(last, 1, wt)
+                vector_plus_shift(LAST, 1, wt)
+                store_half(out_1, LAST, 1, wt, xn_of(LAST))
 
         load_g1(0)
         load_weights((0, 1))
@@ -618,7 +641,7 @@ def tile_block_attention_guide_pb_t_kernel(
         load_adj(1)
 
         zero_other_rows()
-        keep_warm(4)
+        keep_warm(WARM_MATMULS)
         for half in range(2):
             turn_g1(0, half)
             group_g1(0, half)

from contextlib import ExitStack

import concourse.mybir as mybir
from concourse.masks import make_identity

F32 = mybir.dt.float32
BF16 = mybir.dt.bfloat16
U32 = mybir.dt.uint32
U8 = mybir.dt.uint8
I32 = mybir.dt.int32
FP8X4 = mybir.dt.float8_e4m3fn_x4
ALU = mybir.AluOpType
ACT = mybir.ActivationFunctionType

B = 16
J = 256
C = 512
K = 2
EPS = 1e-5
P = 128
PAIRS = B // 2
LAST = PAIRS - 1
HALF = P // 2
PACK = 4
CHUNKS = C // P
A_WORDS = J + J // PACK
W_PARTS = 4
THIN = 64
WARM_MATMULS = 4
SCALAR_ADJ_PAIRS = 2

FLOPS = 2 * B * J * C * (K * C) + 2 * B * (K * J) * J * C


def tile_block_attention_guide_pb_t_kernel(
    tc, g1, res1, adj, spatial_adj, conv2_w, conv2_b, s2, norm2_g, norm2_b, out_0, out_1
):
    nc = tc.nc
    with ExitStack() as ctx:
        consts = ctx.enter_context(tc.tile_pool(name="consts", bufs=1))
        inputs = ctx.enter_context(tc.tile_pool(name="inputs", bufs=4))
        stage = ctx.enter_context(tc.tile_pool(name="stage", bufs=2))
        packed = ctx.enter_context(tc.tile_pool(name="packed", bufs=3))
        results = ctx.enter_context(tc.tile_pool(name="results", bufs=4))
        stats = ctx.enter_context(tc.tile_pool(name="stats", bufs=6))
        psum_turn = ctx.enter_context(tc.psum_pool(name="psum_turn", bufs=2))
        psum_h = ctx.enter_context(tc.psum_pool(name="psum_h", bufs=4))
        psum_g2 = ctx.enter_context(tc.psum_pool(name="psum_g2", bufs=2))
        ctx.enter_context(tc.manual_schedule())

        identity = consts.tile([P, P], F32)
        make_identity(nc, identity[:])
        eps = consts.tile([P, 1], F32)
        nc.vector.memset(eps[:], EPS)

        vector_rows = consts.tile([P, 4 * C + THIN], BF16)
        nc.vector.memset(vector_rows[:].bitcast(I32), 0)
        ones = consts.tile([P, C], BF16)
        nc.vector.memset(ones[:], 1.0)

        def load_vector(vector, column):
            row = vector.rearrange("(o n) -> o n", o=1)
            nc.sync.dma_start(out=vector_rows[0:1, column : column + row.shape[1]], in_=row)

        first_root = consts.tile([P, 1], F32)
        nc.scalar.activation(out=first_root[:], in_=eps[:], func=ACT.Abs_reciprocal_sqrt)

        bias = consts.tile([P, K * C], BF16)
        gain = consts.tile([P, C], BF16)
        shift = consts.tile([P, C], BF16)
        s2_f32 = consts.tile([P, 1], F32)
        columns = consts.tile([P, 2 * CHUNKS], F32)

        def keep_warm(times):
            unread = psum_g2.tile([P, C], F32, tag="g2_acc")
            for n in range(times):
                nc.tensor.matmul(out=unread[:], lhsT=ones[:, 0:P], rhs=ones[:], start=True, stop=True)

        def spread_bias():
            for k in range(K):
                spread = psum_g2.tile([P, C], F32, tag="g2_acc")
                cols = slice(k * C, (k + 1) * C)
                nc.tensor.matmul(
                    out=spread[:], lhsT=ones[:, 0:P], rhs=vector_rows[:, cols], start=True, stop=True
                )
                nc.scalar.copy(out=bias[:, cols], in_=spread[:])

        def spread_s2():
            spread = psum_g2.tile([P, THIN], F32, tag="g2_acc")
            nc.tensor.matmul(
                out=spread[:], lhsT=ones[:, 0:P], rhs=vector_rows[:, 4 * C :], start=True, stop=True
            )
            nc.scalar.copy(out=s2_f32[:], in_=spread[:, 0:1])

        def spread_norm():
            spread = psum_turn.tile([P, 2 * CHUNKS, THIN], F32, tag="turned")
            for n in range(2 * CHUNKS):
                row = vector_rows[:, 2 * C + n * P : 2 * C + (n + 1) * P]
                nc.tensor.matmul(out=spread[:, n, :], lhsT=row, rhs=ones[:, 0:THIN], start=True, stop=True)
            nc.scalar.copy(out=columns[:], in_=spread[:, :, 0])
            for n, spread_to in ((2, gain), (3, shift)):
                spread = psum_turn.tile([P, C], F32, tag="turned")
                cols = slice(n * C, (n + 1) * C)
                nc.tensor.matmul(
                    out=spread[:], lhsT=ones[:, 0:P], rhs=vector_rows[:, cols], start=True, stop=True
                )
                nc.scalar.copy(out=spread_to[:], in_=spread[:])

        w_raw = consts.tile([P, W_PARTS, 2, C], BF16)
        w_grouped = consts.tile([P, K * C * PACK], BF16, align_bytes=64)
        w_codes = consts.tile([P, K * C], U32, align_bytes=64)
        w_scales = consts.tile([P, K * C], U8, align_bytes=64)

        def load_weights(parts):
            for n in parts:
                nc.sync.dma_start(
                    out=w_raw[:, n],
                    in_=conv2_w.rearrange("(n m p) c -> n p m c", n=W_PARTS, p=P)[n],
                )

        def turn_weights(parts):
            for n in parts:
                if n < W_PARTS // K:
                    turned_w = psum_h.tile([P, 2, 2, P], F32, tag="h_acc")
                else:
                    turned_w = psum_turn.tile([P, 2, 2, P], F32, tag="turned")
                for m in range(2):
                    for u in range(2):
                        nc.tensor.transpose(
                            turned_w[:, m, u, :],
                            w_raw[:, n, m, :].bitcast(F32)[:, u : 2 * P : 2],
                            identity[:],
                        )
                width = K * C * PACK // W_PARTS
                cols = slice(n * width, (n + 1) * width)
                words_out = w_grouped[:, cols].bitcast(F32).rearrange("q (m p u) -> q m p u", m=2, u=2)
                words_in = turned_w[:].rearrange("q m u p -> q m p u")
                if n == 0:
                    nc.vector.tensor_copy(out=words_out, in_=words_in)
                else:
                    nc.scalar.copy(out=words_out, in_=words_in)

        def quantise_weights(k):
            nc.vector.quantize_mx(
                out=w_codes[:, k * C : (k + 1) * C].bitcast(FP8X4),
                scales=w_scales[:, k * C : (k + 1) * C],
                in_=w_grouped[:, k * C * PACK : (k + 1) * C * PACK],
            )

        adj_packed = [
            consts.tile([P, A_WORDS], U32, name="adj_packed%d" % n, align_bytes=64) for n in range(2)
        ]
        adj_padded = [
            consts.tile([P, 2, A_WORDS], U32, name="adj_padded%d" % n, align_bytes=64) for n in range(2)
        ]
        spatial_packed = consts.tile([P, A_WORDS], U32, align_bytes=64)
        spatial_padded = consts.tile([P, 2, A_WORDS], U32, align_bytes=64)
        spatial_raw = consts.tile([P, PACK, J], BF16)
        spatial_grouped = consts.tile([P, J, PACK], BF16, align_bytes=64)

        def own_rows(s):
            return slice(s * HALF, (s + 1) * HALF)

        def zero_other_rows():
            for tile in (spatial_packed, adj_packed[0], adj_packed[1]):
                nc.gpsimd.memset(tile[:, J:].bitcast(I32), 0)
            for tile in (spatial_padded, adj_padded[0], adj_padded[1]):
                for s in range(2):
                    nc.gpsimd.memset(tile[own_rows(1 - s), s].bitcast(I32), 0)

        def quantise_a(grouped, tile, padded):
            nc.vector.quantize_mx(
                out=tile[:, 0:J].bitcast(FP8X4),
                scales=tile[:, J:].bitcast(U8),
                in_=grouped[:].rearrange("p w t -> p (w t)"),
            )
            for s in range(2):
                rows = own_rows(s)
                nc.sync.dma_start(out=padded[rows, s].bitcast(I32), in_=tile[rows].bitcast(I32))

        def load_spatial():
            for s in range(2):
                nc.sync.dma_start(
                    out=spatial_raw[own_rows(s)],
                    in_=spatial_adj[0].rearrange("(r t) w -> r t w", t=PACK),
                )

        def place_spatial():
            nc.scalar.copy(
                out=spatial_grouped[:].rearrange("p (wt m) t -> p wt m t", wt=2),
                in_=spatial_raw[:].rearrange("p t (m wt) -> p wt m t", wt=2),
            )

        g1_raw = {}
        res_raw = {}
        adj_raw = {}
        g1_turned = {}
        g1_grouped = {}
        g1_codes = {}
        g1_scales = {}
        adj_grouped = {}
        h_acc = {}
        h_grouped = {}
        h_codes = {}
        h_scales = {}
        g2_acc = {}
        x2 = {}
        row_sum = {}
        neg_mean = {}
        squares = {}
        rstd = {}
        offset = {}
        scaled_xn = {}
        xn_tile = {}

        def load_g1(i):
            g1_raw[i] = inputs.tile([P, PACK, C], BF16, tag="g1_raw", name="g1_raw%d" % i)
            rows = g1[2 * i : 2 * i + 2].rearrange("b (r t) c -> (b r) t c", t=PACK)
            if i == 0:
                for half in range(2):
                    part = slice(2 * half, 2 * half + 2)
                    nc.sync.dma_start(out=g1_raw[i][:, part], in_=rows[:, part])
            else:
                nc.sync.dma_start(out=g1_raw[i][:], in_=rows)

        def load_adj(i):
            adj_raw[i] = inputs.tile([P, PACK, J], BF16, tag="adj_raw", name="adj_raw%d" % i)
            nc.sync.dma_start(
                out=adj_raw[i][:], in_=adj[2 * i : 2 * i + 2, 0].rearrange("b (r t) w -> (b r) t w", t=PACK)
            )

        def load_res(i):
            res_raw[i] = inputs.tile([P, 2, 2, C], BF16, tag="res_raw", name="res_raw%d" % i)
            nc.sync.dma_start(
                out=res_raw[i][:].rearrange("p s wt c -> p s (wt c)"),
                in_=res1[2 * i : 2 * i + 2].rearrange("s (m wt) c -> m s (wt c)", wt=2),
            )

        def turn_g1(i, half):
            turned = psum_turn.tile([P, 2, 2, P], F32, tag="turned")
            for t in range(2):
                for u in range(2):
                    nc.tensor.transpose(
                        turned[:, t, u, :],
                        g1_raw[i][:, 2 * half + t, :].bitcast(F32)[:, u : 2 * P : 2],
                        identity[:],
                    )
            g1_turned[(i, half)] = turned

        def group_g1(i, half):
            if half == 0:
                grouped = stage.tile([P, PACK * P * PACK], BF16, tag="g1_grouped", align_bytes=64)
                g1_grouped[i] = grouped
            cols = slice(half * 2 * P * PACK, (half + 1) * 2 * P * PACK)
            nc.scalar.copy(
                out=g1_grouped[i][:, cols].bitcast(F32).rearrange("q (t n u) -> q t n u", t=2, u=2),
                in_=g1_turned[(i, half)][:].rearrange("q t u n -> q t n u"),
            )

        def quantise_g1(i):
            codes = packed.tile([P, PACK * P], U32, tag="g1_codes", align_bytes=64)
            scales = packed.tile([P, PACK * P], U8, tag="g1_scales", align_bytes=64)
            nc.vector.quantize_mx(out=codes[:].bitcast(FP8X4), scales=scales[:], in_=g1_grouped[i][:])
            g1_codes[i] = codes
            g1_scales[i] = scales

        def scale_adj(i):
            grouped = stage.tile([P, J, PACK], BF16, tag="adj_grouped", align_bytes=64)
            source = adj_raw[i][:].rearrange("p t (m wt) -> p wt m t", wt=2)
            target = grouped[:].rearrange("p (wt m) t -> p wt m t", wt=2)
            if i < SCALAR_ADJ_PAIRS:
                nc.scalar.activation(out=target, in_=source, func=ACT.Copy, scale=s2_f32[:])
            else:
                nc.gpsimd.tensor_scalar(
                    out=target, in0=source, scalar1=s2_f32[:], scalar2=0.0, op0=ALU.mult, op1=ALU.add
                )
            adj_grouped[i] = grouped

        def conv(i, k, cc):
            acc = psum_h.tile([P, PACK, P], F32, tag="h_acc")
            w_cols = slice(k * C + cc * P, k * C + (cc + 1) * P)
            for t in range(PACK):
                cols = slice(t * P, (t + 1) * P)
                nc.tensor.matmul_mx(
                    out=acc[:, t, :],
                    lhsT=g1_codes[i][:, cols].bitcast(FP8X4),
                    lhsT_scale=g1_scales[i][:, cols],
                    rhs=w_codes[:, w_cols].bitcast(FP8X4),
                    rhs_scale=w_scales[:, w_cols],
                    start=True,
                    stop=True,
                )
            h_acc[(i, k, cc)] = acc

        def add_bias(i, k, cc):
            if cc == 0:
                grouped = stage.tile([P, C, PACK], BF16, tag="h_grouped%d" % k, align_bytes=64)
                h_grouped[(i, k)] = grouped
            cols = slice(cc * P, (cc + 1) * P)
            nc.vector.tensor_tensor(
                out=h_grouped[(i, k)][:, cols, :],
                in0=h_acc[(i, k, cc)][:].rearrange("p t c -> p c t"),
                in1=bias[:, k * C + cc * P : k * C + (cc + 1) * P].unsqueeze(2).to_broadcast([P, P, PACK]),
                op=ALU.add,
            )

        def quantise_h(i, k):
            codes = packed.tile([P, C], U32, tag="h_codes%d" % k, align_bytes=64)
            scales = packed.tile([P, C], U8, tag="h_scales%d" % k, align_bytes=64)
            nc.vector.quantize_mx(
                out=codes[:].bitcast(FP8X4),
                scales=scales[:],
                in_=h_grouped[(i, k)][:].rearrange("p c t -> p (c t)"),
            )
            h_codes[(i, k)] = codes
            h_scales[(i, k)] = scales

        def aggregate(i, s):
            for wt in range(2):
                cols = slice(wt * P, (wt + 1) * P)
                acc = psum_g2.tile([P, C], F32, tag="g2_acc")
                for k, padded in enumerate((adj_padded[i % 2], spatial_padded)):
                    nc.tensor.matmul_mx(
                        out=acc[:],
                        lhsT=padded[:, s, cols].bitcast(FP8X4),
                        lhsT_scale=padded[:, s, J:].bitcast(U8)[:, cols],
                        rhs=h_codes[(i, k)][:].bitcast(FP8X4),
                        rhs_scale=h_scales[(i, k)][:],
                        start=(k == 0),
                        stop=(k == K - 1),
                    )
                g2_acc[(i, s, wt)] = acc

        def add_residual(i, s):
            if s == 0:
                x2_tile = results.tile([P, 2, 2, C], F32, tag="x2")
                x2[i] = x2_tile
                sums = stats.tile([P, 2, 2], F32, tag="row_sum")
                row_sum[i] = sums
            for wt in range(2):
                nc.vector.scalar_tensor_tensor(
                    out=x2[i][:, s, wt, :],
                    in0=g2_acc[(i, s, wt)][:],
                    scalar=1.0,
                    in1=res_raw[i][:, s, wt, :],
                    op0=ALU.mult,
                    op1=ALU.add,
                    accum_out=row_sum[i][:, s, wt : wt + 1],
                )
            if i == LAST:
                store_sample(out_0, i, s, x2[i])
            elif s == 1:
                store_pair(out_0, i, x2[i])

        def store_pair(out, i, tile):
            nc.sync.dma_start(
                out=out[2 * i : 2 * i + 2].rearrange("s (m wt) c -> m s (wt c)", wt=2),
                in_=tile[:].rearrange("p s wt c -> p s (wt c)"),
            )

        def store_sample(out, i, s, tile):
            nc.sync.dma_start(out=out[2 * i + s].rearrange("(m wt) c -> m wt c", wt=2), in_=tile[:, s])

        def store_half(out, i, s, wt, tile):
            nc.sync.dma_start(
                out=out[2 * i + s].rearrange("(m wt) c -> wt m c", wt=2)[wt], in_=tile[:, s, wt, :]
            )

        BOTH = slice(0, 2)

        def negate_mean(i, s):
            if i not in neg_mean:
                minus_mean = stats.tile([P, 2, 2], F32, tag="neg_mean")
                neg_mean[i] = minus_mean
            nc.scalar.activation(
                out=neg_mean[i][:, s, :], in_=row_sum[i][:, s, :], func=ACT.Copy, scale=-1.0 / C
            )

        def square(i, s):
            if i not in squares:
                sums = stats.tile([P, 2, 2], F32, tag="squares")
                squares[i] = sums
            for wt in range(2):
                unread = stats.tile([P, C], BF16, tag="unread")
                nc.scalar.activation(
                    out=unread[:],
                    in_=x2[i][:, s, wt, :],
                    func=ACT.Square,
                    bias=neg_mean[i][:, s, wt : wt + 1],
                    scale=1.0,
                    accum_out=squares[i][:, s, wt : wt + 1],
                )

        def root(i, s):
            if i not in rstd:
                inverse = stats.tile([P, 2, 2], F32, tag="rstd")
                rstd[i] = inverse
            nc.scalar.activation(
                out=rstd[i][:, s, :],
                in_=squares[i][:, s, :],
                func=ACT.Abs_reciprocal_sqrt,
                bias=eps[:],
                scale=1.0 / C,
            )

        def offset_mean(i):
            product = stats.tile([P, 2, 2], F32, tag="offset")
            nc.vector.tensor_tensor(out=product[:], in0=neg_mean[i][:], in1=rstd[i][:], op=ALU.mult)
            offset[i] = product

        def xn_of(i):
            if i not in xn_tile:
                xn = results.tile([P, 2, 2, C], F32, tag="xn")
                xn_tile[i] = xn
            return xn_tile[i]

        def vector_times_gain(i, s, wt):
            nc.vector.scalar_tensor_tensor(
                out=xn_of(i)[:, s, wt, :],
                in0=x2[i][:, s, wt, :],
                scalar=neg_mean[i][:, s, wt : wt + 1],
                in1=gain[:],
                op0=ALU.add,
                op1=ALU.mult,
            )

        def vector_plus_shift(i, s, wt):
            nc.vector.scalar_tensor_tensor(
                out=xn_of(i)[:, s, wt, :],
                in0=xn_of(i)[:, s, wt, :],
                scalar=rstd[i][:, s, wt : wt + 1],
                in1=shift[:],
                op0=ALU.mult,
                op1=ALU.add,
            )

        def standardise(i, s, wt):
            nc.scalar.activation(
                out=xn_of(i)[:, s, wt, :],
                in_=x2[i][:, s, wt, :],
                func=ACT.Identity,
                bias=offset[i][:, s, wt : wt + 1],
                scale=rstd[i][:, s, wt : wt + 1],
            )

        def turn_forth(i, s, wt):
            turned = psum_turn.tile([P, CHUNKS, P], F32, tag="turned")
            for cc in range(CHUNKS):
                nc.tensor.transpose(turned[:, cc, :], xn_of(i)[:, s, wt, cc * P : (cc + 1) * P], identity[:])
            scaled = stage.tile([P, CHUNKS, P], F32, tag="scaled%d%d" % (s, wt))
            for cc in range(CHUNKS):
                nc.scalar.activation(
                    out=scaled[:, cc, :],
                    in_=turned[:, cc, :],
                    func=ACT.Identity,
                    bias=columns[:, CHUNKS + cc : CHUNKS + cc + 1],
                    scale=columns[:, cc : cc + 1],
                )
            scaled_xn[(i, s, wt)] = scaled[:]

        def turn_forth_both(i):
            scaled = stage.tile([P, CHUNKS, 2, P], F32, tag="scaled_both")
            for half in range(2):
                turned = psum_turn.tile([P, 2, 2, P], F32, tag="turned")
                for n in range(2):
                    cc = 2 * half + n
                    for wt in range(2):
                        nc.tensor.transpose(
                            turned[:, n, wt, :], xn_of(i)[:, 1, wt, cc * P : (cc + 1) * P], identity[:]
                        )
                for n in range(2):
                    cc = 2 * half + n
                    nc.scalar.activation(
                        out=scaled[:, cc],
                        in_=turned[:, n],
                        func=ACT.Identity,
                        bias=columns[:, CHUNKS + cc : CHUNKS + cc + 1],
                        scale=columns[:, cc : cc + 1],
                    )
            for wt in range(2):
                scaled_xn[(i, 1, wt)] = scaled[:, :, wt, :]

        def turn_back(i, s, wt):
            turned = psum_turn.tile([P, CHUNKS, P], F32, tag="turned")
            for cc in range(CHUNKS):
                nc.tensor.transpose(turned[:, cc, :], scaled_xn[(i, s, wt)][:, cc, :], identity[:])
            nc.scalar.copy(out=xn_of(i)[:, s, wt, :], in_=turned[:].rearrange("p c n -> p (c n)"))

        def gpsimd_apply(i, s, wts, vector, op):
            part = xn_of(i)[:, s, wts, :]
            many = wts.stop - wts.start
            nc.gpsimd.tensor_tensor(
                out=part, in0=part, in1=vector[:].unsqueeze(1).to_broadcast([P, many, C]), op=op
            )

        def apply_on_vector(i, s, wts):
            for wt in wts:
                vector_times_gain(i, s, wt)
            for wt in wts:
                vector_plus_shift(i, s, wt)

        def in_range(i):
            return 0 <= i < PAIRS

        def first_step():
            load_g1(3)
            load_adj(2)
            load_res(1)
            for cc in range(CHUNKS):
                add_bias(0, 0, cc)
            quantise_a(adj_grouped[0], adj_packed[0], adj_padded[0])
            quantise_weights(1)
            for cc in range(CHUNKS):
                conv(0, 1, cc)
            for half in range(2):
                turn_g1(1, half)
                group_g1(1, half)
            scale_adj(1)
            for cc in range(CHUNKS):
                add_bias(0, 1, cc)
                if cc == 1:
                    quantise_a(spatial_grouped, spatial_packed, spatial_padded)
            quantise_h(0, 0)
            quantise_h(0, 1)
            aggregate(0, 0)
            quantise_g1(1)
            for cc in range(CHUNKS):
                conv(1, 0, cc)
            for half in range(2):
                turn_g1(2, half)
                group_g1(2, half)
            quantise_a(adj_grouped[1], adj_packed[1], adj_padded[1])

        def step(i):
            last = i == LAST
            done = i - 2
            if in_range(i + 3):
                load_g1(i + 3)
            if in_range(i + 2):
                load_adj(i + 2)
            if not last:
                load_res(i + 1)
            if in_range(done):
                for s in range(2):
                    for wt in range(2):
                        standardise(done, s, wt)
                gpsimd_apply(done, 0, slice(0, 1), gain, ALU.mult)
                gpsimd_apply(done, 0, slice(1, 2), gain, ALU.mult)
                gpsimd_apply(done, 0, slice(0, 2), shift, ALU.add)
            for n in range(K * CHUNKS):
                k, cc = divmod(n, CHUNKS)
                add_bias(i, k, cc)
                if k == 0:
                    conv(i, 1, cc)
                elif not last:
                    conv(i + 1, 0, cc)
                if n == 0 and i > 1 and not last:
                    scale_adj(i + 1)
                if n == 0 and in_range(done - 1):
                    for wt in range(2):
                        turn_back(done - 1, 1, wt)
                    store_pair(out_1, done - 1, xn_of(done - 1))
                if n == 1:
                    add_residual(i - 1, 0)
                    aggregate(i - 1, 1)
                    negate_mean(i - 1, 0)
                    square(i - 1, 0)
                if n == 2 and in_range(i + 2):
                    for half in range(2):
                        turn_g1(i + 2, half)
                        group_g1(i + 2, half)
                if n == 3 and i == 1:
                    quantise_g1(2)
                    scale_adj(2)
                if n == (2 if last else 4):
                    add_residual(i - 1, 1)
                    negate_mean(i - 1, 1)
                    square(i - 1, 1)
                    root(i - 1, BOTH)
                    if in_range(done):
                        turn_forth_both(done)
                if n == 5 and i == 1:
                    spread_norm()
                if n == 6 and last:
                    for wt in range(2):
                        turn_back(done, 1, wt)
                    store_pair(out_1, done, xn_of(done))
                    offset_mean(i - 1)
                    for s, wt in ((0, 1), (0, 0), (1, 1)):
                        standardise(i - 1, s, wt)
                    gpsimd_apply(i - 1, 0, slice(1, 2), gain, ALU.mult)
                    gpsimd_apply(i - 1, 0, slice(1, 2), shift, ALU.add)
            quantise_h(i, 0)
            quantise_h(i, 1)
            aggregate(i, 0)
            if in_range(i + 2):
                quantise_g1(i + 2)
            if not last:
                offset_mean(i - 1)
                quantise_a(adj_grouped[i + 1], adj_packed[(i + 1) % 2], adj_padded[(i + 1) % 2])

        def finish():
            done = LAST - 1
            add_residual(LAST, 0)
            aggregate(LAST, 1)
            negate_mean(LAST, 0)
            square(LAST, 0)
            root(LAST, 0)
            turn_forth(done, 0, 0)
            add_residual(LAST, 1)
            negate_mean(LAST, 1)
            square(LAST, 1)
            root(LAST, 1)
            apply_on_vector(LAST, 0, (0, 1))
            store_sample(out_1, LAST, 0, xn_of(LAST))
            turn_forth(done, 1, 1)
            turn_back(done, 0, 0)
            store_sample(out_1, done, 0, xn_of(done))
            vector_times_gain(done, 1, 0)
            vector_times_gain(LAST, 1, 0)
            vector_plus_shift(done, 1, 0)
            turn_back(done, 1, 1)
            store_sample(out_1, done, 1, xn_of(done))
            vector_times_gain(LAST, 1, 1)
            for wt in range(2):
                vector_plus_shift(LAST, 1, wt)
                store_half(out_1, LAST, 1, wt, xn_of(LAST))

        load_g1(0)
        load_weights((0, 1))
        load_vector(conv2_b, 0)
        load_vector(s2, 4 * C)
        load_weights((2, 3))
        load_adj(0)
        load_spatial()
        load_g1(1)
        load_vector(norm2_g, 2 * C)
        load_vector(norm2_b, 3 * C)
        load_res(0)
        load_g1(2)
        load_adj(1)

        zero_other_rows()
        keep_warm(WARM_MATMULS)
        for half in range(2):
            turn_g1(0, half)
            group_g1(0, half)
        turn_weights((0, 1))
        quantise_g1(0)
        quantise_weights(0)
        spread_bias()
        spread_s2()
        for cc in range(CHUNKS):
            conv(0, 0, cc)
        scale_adj(0)
        turn_weights((2, 3))
        place_spatial()
        first_step()
        for i in range(1, PAIRS):
            step(i)
        finish()
